import numpy as np
import ml_dtypes


def mxq(x, axis, fmt="e4m3"):
    dtype, down = {"e4m3": (ml_dtypes.float8_e4m3fn, 7), "e5m2": (ml_dtypes.float8_e5m2, 14)}[fmt]
    v = np.moveaxis(np.asarray(x, np.float32).astype(ml_dtypes.bfloat16).astype(np.float64), axis, -1)
    blocks = v.reshape(v.shape[:-1] + (-1, 32))
    amax = np.abs(blocks).max(-1, keepdims=True)
    byte = np.maximum(np.where(amax > 0, np.frexp(amax)[1] - 1 + 127, 0) - down, 1)
    scale = np.exp2(byte - 127.0)
    codes = (blocks / scale).astype(np.float32).astype(dtype).astype(np.float64)
    return np.moveaxis((codes * scale).reshape(v.shape), -1, axis)


WIDE = False


def mx_kscale(k):
    if not WIDE:
        return np.ones(k)
    levels = np.array([10, -10, 5, -5, 0])
    a = np.random.permutation(np.resize(levels, k // 512 * 4)).reshape(k // 512, 4)
    idx = np.arange(k)
    return np.exp2(a[idx // 512, idx % 128 // 32])


BF16 = ml_dtypes.bfloat16


def bf(x):
    return np.asarray(x, np.float32).astype(BF16)


def f64(x):
    return np.asarray(x).astype(np.float64)


B, T, C, CO, HS, DW, DA, DV, DG = 4, 1024, 1024, 256, 64, 128, 128, 128, 128
H = C // HS
EPS_GN = 0.00064


def setup_inputs():
    n = np.random.standard_normal
    t = mx_kscale(C)
    return {
        "y": bf(n((B, T, C)) * 0.1),
        "r": bf(n((B, T, C))),
        "k": bf(n((B, T, C)) * 0.6),
        "v": bf(n((B, T, C)) * 0.8),
        "g_hid": bf(1.0 / (1.0 + np.exp(-n((B, T, DG))))),
        "g2": bf(n((DG, C)) * 2.0 / np.sqrt(DG) * t),
        "r_k": bf(n((H, HS)) * 0.2 - 0.04),
        "ln_g": bf(1.0 + n((C,)) * 0.1),
        "ln_b": bf(n((C,)) * 0.1),
        "W_o": bf(n((CO, C)) * 0.7 / np.sqrt(C) / t),
    }


def reference(y, r, k, v, g_hid, g2, r_k, ln_g, ln_b, W_o):
    yh = f64(y).reshape(B, T, H, HS)
    mu = np.mean(yh, axis=-1, keepdims=True)
    var = np.mean((yh - mu) ** 2, axis=-1, keepdims=True)
    yn = ((yh - mu) / np.sqrt(var + EPS_GN)).reshape(B, T, C)
    yn = yn * f64(ln_g) + f64(ln_b)
    rh = f64(r).reshape(B, T, H, HS)
    kh = f64(k).reshape(B, T, H, HS)
    vh = f64(v).reshape(B, T, H, HS)
    dot = np.sum(rh * kh * f64(r_k), axis=-1, keepdims=True)
    y2 = yn + (dot * vh).reshape(B, T, C)
    g = f64(g_hid) @ f64(g2)
    z = y2 * g
    return mxq(z, 2, "e4m3") @ mxq(f64(W_o), 1, "e4m3").T

@@ -1,0 +1,221 @@
+from contextlib import ExitStack
+
+import concourse.mybir as mybir
+from concourse.masks import make_identity
+
+F32 = mybir.dt.float32
+BF16 = mybir.dt.bfloat16
+U32 = mybir.dt.uint32
+U8 = mybir.dt.uint8
+FP8X4 = mybir.dt.float8_e4m3fn_x4
+ALU = mybir.AluOpType
+ACTF = mybir.ActivationFunctionType
+AX = mybir.AxisListType
+
+P = 128
+TOK = 4096
+C = 1024
+CO = 256
+HS = 64
+H = C // HS
+DG = 128
+EPS_GN = 0.00064
+J = 4
+S = TOK // (P * J)
+NPASS = C // 512
+
+FLOPS = 2 * TOK * DG * C + 2 * TOK * C * CO
+
+
+def tile_full_tmix_params_pc_t_kernel(tc, y, r, k, v, g_hid, g2, r_k, ln_g, ln_b, W_o, out):
+    nc = tc.nc
+
+    def tok_view(x):
+        return x.flatten_outer_dims().rearrange("(s p j) c -> s p (j c)", p=P, j=J)
+
+    y_v = tok_view(y)
+    r_v = tok_view(r)
+    k_v = tok_view(k)
+    v_v = tok_view(v)
+    out_v = out.flatten_outer_dims().rearrange("(s p j) o -> s p j o", p=P, j=J)
+
+    with ExitStack() as ctx:
+        const = ctx.enter_context(tc.tile_pool(name="const", bufs=1))
+        inp = ctx.enter_context(tc.tile_pool(name="inp", bufs=3))
+        work = ctx.enter_context(tc.tile_pool(name="work", bufs=3))
+        small = ctx.enter_context(tc.tile_pool(name="small", bufs=2))
+        psum = ctx.enter_context(tc.psum_pool(name="psum", bufs=2))
+
+        ident_f = const.tile([P, P], F32)
+        make_identity(nc, ident_f[:])
+        ident_b = const.tile([P, P], BF16)
+        make_identity(nc, ident_b[:])
+
+        rows = const.tile([P, P], BF16)
+        nc.gpsimd.memset(rows[:], 0.0)
+        nc.scalar.dma_start(out=rows[0:8, :], in_=ln_g.rearrange("(a c) -> a c", c=P))
+        nc.scalar.dma_start(out=rows[8:16, :], in_=ln_b.rearrange("(a c) -> a c", c=P))
+        g2_sb = const.tile([P, C], BF16)
+        nc.scalar.dma_start(out=g2_sb[:], in_=g2)
+        w_raw = const.tile([P, 2, C], BF16)
+        nc.scalar.dma_start(out=w_raw[:], in_=W_o.rearrange("(a p) c -> p a c", p=P))
+        rk_b = const.tile([P, C], BF16)
+        nc.scalar.dma_start(out=rk_b[:], in_=r_k.rearrange("h c -> (h c)").partition_broadcast(P))
+        gh = const.tile([P, S, J * DG], BF16)
+        nc.scalar.dma_start(
+            out=gh[:], in_=g_hid.flatten_outer_dims().rearrange("(s p j) d -> p s (j d)", p=P, j=J)
+        )
+
+        rows_t = psum.tile([P, P], BF16, tag="misc", bufs=1)
+        nc.tensor.transpose(rows_t[:], rows[:], ident_b[:])
+        lgb = const.tile([P, 16], F32)
+        nc.vector.tensor_copy(out=lgb[:], in_=rows_t[:, 0:16])
+
+        w_codes = const.tile([P, NPASS * CO], U32, align_bytes=64)
+        w_scales = const.tile([P, NPASS * CO], U8, align_bytes=64)
+        for g in range(NPASS):
+            w_t = psum.tile([P, 4, CO], BF16, tag="misc", bufs=1)
+            for t in range(4):
+                for a in range(2):
+                    cb = g * 4 + t
+                    nc.tensor.transpose(
+                        w_t[:, t, a * P : (a + 1) * P], w_raw[:, a, cb * P : (cb + 1) * P], ident_b[:]
+                    )
+            w_grp = const.tile([P, CO, 4], BF16, align_bytes=64)
+            nc.vector.tensor_copy(out=w_grp[:], in_=w_t[:].rearrange("p t o -> p o t"))
+            nc.vector.quantize_mx(
+                out=w_codes[:, g * CO : (g + 1) * CO].bitcast(FP8X4),
+                scales=w_scales[:, g * CO : (g + 1) * CO],
+                in_=w_grp[:].rearrange("p o t -> p (o t)"),
+            )
+
+        for s in range(S):
+            r_t = inp.tile([P, J * C], BF16)
+            nc.sync.dma_start(out=r_t[:], in_=r_v[s])
+            k_t = inp.tile([P, J * C], BF16)
+            nc.sync.dma_start(out=k_t[:], in_=k_v[s])
+            y_t = inp.tile([P, J * C], BF16)
+            nc.sync.dma_start(out=y_t[:], in_=y_v[s])
+            v_t = inp.tile([P, J * C], BF16)
+            nc.sync.dma_start(out=v_t[:], in_=v_v[s])
+
+            gh_ps = psum.tile([P, J, P], BF16, tag="misc", bufs=1)
+            for j in range(J):
+                nc.tensor.transpose(gh_ps[:, j, :], gh[:, s, j * DG : (j + 1) * DG], ident_b[:])
+            gh_t = small.tile([P, J, P], BF16)
+            nc.vector.tensor_copy(out=gh_t[:], in_=gh_ps[:])
+
+            st = small.tile([P, J * H * 3], F32)
+            dot = small.tile([P, J * H], F32)
+            for j in range(J):
+                q = work.tile([P, C], F32)
+                nc.gpsimd.tensor_tensor(
+                    out=q[:], in0=r_t[:, j * C : (j + 1) * C], in1=k_t[:, j * C : (j + 1) * C], op=ALU.mult
+                )
+                nc.gpsimd.tensor_tensor(out=q[:], in0=q[:], in1=rk_b[:], op=ALU.mult)
+                for hp in range(H // 2):
+                    c0 = j * C + hp * 2 * HS
+                    i0 = (j * (H // 2) + hp) * 6
+                    nc.vector.bn_stats(
+                        out=st[:, i0 : i0 + 6],
+                        in_=y_t[:, c0 : c0 + 2 * HS].rearrange("p (h c) -> p c h", h=2),
+                    )
+                nc.vector.tensor_reduce(
+                    out=dot[:, j * H : (j + 1) * H],
+                    in_=q[:].rearrange("p (h c) -> p h c", c=HS),
+                    axis=AX.X,
+                    op=ALU.add,
+                )
+
+            st_v = st[:].rearrange("p (n t) -> p n t", t=3)
+            var = small.tile([P, J * H], F32)
+            nc.vector.tensor_scalar(
+                out=var[:], in0=st_v[:, :, 2], scalar1=1.0 / HS, scalar2=EPS_GN, op0=ALU.mult, op1=ALU.add
+            )
+            std = small.tile([P, J * H], F32)
+            nc.scalar.activation(out=std[:], in_=var[:], func=ACTF.Sqrt)
+            rstd = small.tile([P, J * H], F32)
+            nc.vector.reciprocal(out=rstd[:], in_=std[:])
+            shift = small.tile([P, J * H], F32)
+            nc.vector.scalar_tensor_tensor(
+                out=shift[:], in0=st_v[:, :, 1], scalar=-1.0, in1=rstd[:], op0=ALU.mult, op1=ALU.mult
+            )
+
+            for j in range(J):
+                n_t = work.tile([P, C], F32)
+                w_t2 = work.tile([P, C], F32)
+                for h in range(H):
+                    col = j * H + h
+                    src = slice(j * C + h * HS, j * C + (h + 1) * HS)
+                    dst = slice(h * HS, (h + 1) * HS)
+                    nc.scalar.activation(
+                        out=n_t[:, dst],
+                        in_=y_t[:, src],
+                        func=ACTF.Identity,
+                        bias=shift[:, col : col + 1],
+                        scale=rstd[:, col : col + 1],
+                    )
+                    nc.scalar.activation(
+                        out=w_t2[:, dst], in_=v_t[:, src], func=ACTF.Copy, scale=dot[:, col : col + 1]
+                    )
+
+                grp = work.tile([P, NPASS, P, 4], BF16, align_bytes=64)
+                for g in range(NPASS):
+                    n_ps = psum.tile([P, 4, P], F32)
+                    w_ps = psum.tile([P, 4, P], F32)
+                    g_ps = psum.tile([P, 4, P], F32)
+                    for t in range(4):
+                        cb = g * 4 + t
+                        nc.tensor.transpose(n_ps[:, t, :], n_t[:, cb * P : (cb + 1) * P], ident_f[:])
+                    for t in range(4):
+                        cb = g * 4 + t
+                        nc.tensor.transpose(w_ps[:, t, :], w_t2[:, cb * P : (cb + 1) * P], ident_f[:])
+                    for t in range(4):
+                        cb = g * 4 + t
+                        nc.tensor.matmul(
+                            g_ps[:, t, :],
+                            lhsT=g2_sb[:, cb * P : (cb + 1) * P],
+                            rhs=gh_t[:, j, :],
+                            start=True,
+                            stop=True,
+                        )
+                    e_t = work.tile([P, 4, P], F32)
+                    for t in range(4):
+                        cb = g * 4 + t
+                        nc.scalar.activation(
+                            out=e_t[:, t, :],
+                            in_=n_ps[:, t, :],
+                            func=ACTF.Identity,
+                            bias=lgb[:, 8 + cb : 9 + cb],
+                            scale=lgb[:, cb : cb + 1],
+                        )
+                    f_t = work.tile([P, 4, P], F32)
+                    nc.vector.tensor_tensor(out=f_t[:], in0=e_t[:], in1=w_ps[:], op=ALU.add)
+                    nc.vector.tensor_tensor(
+                        out=grp[:, g],
+                        in0=f_t[:].rearrange("p t m -> p m t"),
+                        in1=g_ps[:].rearrange("p t m -> p m t"),
+                        op=ALU.mult,
+                    )
+
+                z_codes = work.tile([P, NPASS * P], U32, align_bytes=64)
+                z_scales = work.tile([P, NPASS * P], U8, align_bytes=64)
+                nc.vector.quantize_mx(
+                    out=z_codes[:].bitcast(FP8X4),
+                    scales=z_scales[:],
+                    in_=grp[:].rearrange("p g m t -> p (g m t)"),
+                )
+                o_ps = psum.tile([P, CO], F32, bufs=1)
+                for g in range(NPASS):
+                    nc.tensor.matmul_mx(
+                        out=o_ps[:],
+                        lhsT=z_codes[:, g * P : (g + 1) * P].bitcast(FP8X4),
+                        lhsT_scale=z_scales[:, g * P : (g + 1) * P],
+                        rhs=w_codes[:, g * CO : (g + 1) * CO].bitcast(FP8X4),
+                        rhs_scale=w_scales[:, g * CO : (g + 1) * CO],
+                        start=(g == 0),
+                        stop=(g == NPASS - 1),
+                    )
+                o_sb = work.tile([P, CO], F32)
+                nc.scalar.copy(out=o_sb[:], in_=o_ps[:])
+                nc.scalar.dma_start(out=out_v[s][:, j, :], in_=o_sb[:])

@@ -20,9 +20,9 @@ HS = 64
 H = C // HS
 DG = 128
 EPS_GN = 0.00064
-J = 4
-S = TOK // (P * J)
 NPASS = C // 512
+JMAX = 4
+BATCHES = (1, 1, 2, 4, 4, 4, 4, 4, 4, 2, 1, 1)
 
 FLOPS = 2 * TOK * DG * C + 2 * TOK * C * CO
 
@@ -30,19 +30,18 @@ FLOPS = 2 * TOK * DG * C + 2 * TOK * C * CO
 def tile_full_tmix_params_pc_t_kernel(tc, y, r, k, v, g_hid, g2, r_k, ln_g, ln_b, W_o, out):
     nc = tc.nc
 
-    def tok_view(x):
-        return x.flatten_outer_dims().rearrange("(s p j) c -> s p (j c)", p=P, j=J)
-
-    y_v = tok_view(y)
-    r_v = tok_view(r)
-    k_v = tok_view(k)
-    v_v = tok_view(v)
-    out_v = out.flatten_outer_dims().rearrange("(s p j) o -> s p j o", p=P, j=J)
+    y_f = y.flatten_outer_dims()
+    r_f = r.flatten_outer_dims()
+    k_f = k.flatten_outer_dims()
+    v_f = v.flatten_outer_dims()
+    gh_f = g_hid.flatten_outer_dims()
+    out_f = out.flatten_outer_dims()
 
     with ExitStack() as ctx:
         const = ctx.enter_context(tc.tile_pool(name="const", bufs=1))
         inp = ctx.enter_context(tc.tile_pool(name="inp", bufs=3))
         work = ctx.enter_context(tc.tile_pool(name="work", bufs=3))
+        big = ctx.enter_context(tc.tile_pool(name="big", bufs=2))
         small = ctx.enter_context(tc.tile_pool(name="small", bufs=2))
         psum = ctx.enter_context(tc.psum_pool(name="psum", bufs=2))
 
@@ -61,10 +60,8 @@ def tile_full_tmix_params_pc_t_kernel(tc, y, r, k, v, g_hid, g2, r_k, ln_g, ln_b
         nc.scalar.dma_start(out=w_raw[:], in_=W_o.rearrange("(a p) c -> p a c", p=P))
         rk_b = const.tile([P, C], BF16)
         nc.scalar.dma_start(out=rk_b[:], in_=r_k.rearrange("h c -> (h c)").partition_broadcast(P))
-        gh = const.tile([P, S, J * DG], BF16)
-        nc.scalar.dma_start(
-            out=gh[:], in_=g_hid.flatten_outer_dims().rearrange("(s p j) d -> p s (j d)", p=P, j=J)
-        )
+        eps_t = const.tile([P, 1], F32)
+        nc.gpsimd.memset(eps_t[:], EPS_GN)
 
         rows_t = psum.tile([P, P], BF16, tag="misc", bufs=1)
         nc.tensor.transpose(rows_t[:], rows[:], ident_b[:])
@@ -89,25 +86,32 @@ def tile_full_tmix_params_pc_t_kernel(tc, y, r, k, v, g_hid, g2, r_k, ln_g, ln_b
                 in_=w_grp[:].rearrange("p o t -> p (o t)"),
             )
 
-        for s in range(S):
-            r_t = inp.tile([P, J * C], BF16)
-            nc.sync.dma_start(out=r_t[:], in_=r_v[s])
-            k_t = inp.tile([P, J * C], BF16)
-            nc.sync.dma_start(out=k_t[:], in_=k_v[s])
-            y_t = inp.tile([P, J * C], BF16)
-            nc.sync.dma_start(out=y_t[:], in_=y_v[s])
-            v_t = inp.tile([P, J * C], BF16)
-            nc.sync.dma_start(out=v_t[:], in_=v_v[s])
+        t0 = 0
+        for nb in BATCHES:
+            def bview(x):
+                return x[t0 : t0 + P * nb, :].rearrange("(p j) c -> p (j c)", j=nb)
 
-            gh_ps = psum.tile([P, J, P], BF16, tag="misc", bufs=1)
-            for j in range(J):
-                nc.tensor.transpose(gh_ps[:, j, :], gh[:, s, j * DG : (j + 1) * DG], ident_b[:])
-            gh_t = small.tile([P, J, P], BF16)
-            nc.vector.tensor_copy(out=gh_t[:], in_=gh_ps[:])
+            r_t = inp.tile([P, JMAX * C], BF16)
+            nc.sync.dma_start(out=r_t[:, : nb * C], in_=bview(r_f))
+            k_t = inp.tile([P, JMAX * C], BF16)
+            nc.sync.dma_start(out=k_t[:, : nb * C], in_=bview(k_f))
+            y_t = inp.tile([P, JMAX * C], BF16)
+            nc.sync.dma_start(out=y_t[:, : nb * C], in_=bview(y_f))
+            v_t = inp.tile([P, JMAX * C], BF16)
+            nc.sync.dma_start(out=v_t[:, : nb * C], in_=bview(v_f))
+            gh = small.tile([P, JMAX * DG], BF16)
+            nc.sync.dma_start(out=gh[:, : nb * DG], in_=bview(gh_f))
 
-            st = small.tile([P, J * H * 3], F32)
-            dot = small.tile([P, J * H], F32)
-            for j in range(J):
+            gh_ps = psum.tile([P, JMAX, P], BF16, tag="misc", bufs=1)
+            for j in range(nb):
+                nc.tensor.transpose(gh_ps[:, j, :], gh[:, j * DG : (j + 1) * DG], ident_b[:])
+            gh_t = small.tile([P, JMAX, P], BF16)
+            nc.vector.tensor_copy(out=gh_t[:, :nb, :], in_=gh_ps[:, :nb, :])
+
+            nh = nb * H
+            st = small.tile([P, JMAX * H * 3], F32)
+            dot = small.tile([P, JMAX * H], F32)
+            for j in range(nb):
                 q = work.tile([P, C], F32)
                 nc.gpsimd.tensor_tensor(
                     out=q[:], in0=r_t[:, j * C : (j + 1) * C], in1=k_t[:, j * C : (j + 1) * C], op=ALU.mult
@@ -128,20 +132,19 @@ def tile_full_tmix_params_pc_t_kernel(tc, y, r, k, v, g_hid, g2, r_k, ln_g, ln_b
                 )
 
             st_v = st[:].rearrange("p (n t) -> p n t", t=3)
-            var = small.tile([P, J * H], F32)
-            nc.vector.tensor_scalar(
-                out=var[:], in0=st_v[:, :, 2], scalar1=1.0 / HS, scalar2=EPS_GN, op0=ALU.mult, op1=ALU.add
+            std = small.tile([P, JMAX * H], F32)
+            nc.scalar.activation(
+                out=std[:, :nh], in_=st_v[:, :nh, 2], func=ACTF.Sqrt, bias=eps_t[:, 0:1], scale=1.0 / HS
             )
-            std = small.tile([P, J * H], F32)
-            nc.scalar.activation(out=std[:], in_=var[:], func=ACTF.Sqrt)
-            rstd = small.tile([P, J * H], F32)
-            nc.vector.reciprocal(out=rstd[:], in_=std[:])
-            shift = small.tile([P, J * H], F32)
-            nc.vector.scalar_tensor_tensor(
-                out=shift[:], in0=st_v[:, :, 1], scalar=-1.0, in1=rstd[:], op0=ALU.mult, op1=ALU.mult
-            )
+            negmean = small.tile([P, JMAX * H], F32)
+            nc.scalar.activation(out=negmean[:, :nh], in_=st_v[:, :nh, 1], func=ACTF.Copy, scale=-1.0)
+            rstd = small.tile([P, JMAX * H], F32)
+            nc.vector.reciprocal(out=rstd[:, :nh], in_=std[:, :nh])
+            shift = small.tile([P, JMAX * H], F32)
+            nc.gpsimd.tensor_tensor(out=shift[:, :nh], in0=negmean[:, :nh], in1=rstd[:, :nh], op=ALU.mult)
 
-            for j in range(J):
+            grp = big.tile([P, JMAX, NPASS, P, 4], BF16, align_bytes=64)
+            for j in range(nb):
                 n_t = work.tile([P, C], F32)
                 w_t2 = work.tile([P, C], F32)
                 for h in range(H):
@@ -159,7 +162,6 @@ def tile_full_tmix_params_pc_t_kernel(tc, y, r, k, v, g_hid, g2, r_k, ln_g, ln_b
                         out=w_t2[:, dst], in_=v_t[:, src], func=ACTF.Copy, scale=dot[:, col : col + 1]
                     )
 
-                grp = work.tile([P, NPASS, P, 4], BF16, align_bytes=64)
                 for g in range(NPASS):
                     n_ps = psum.tile([P, 4, P], F32)
                     w_ps = psum.tile([P, 4, P], F32)
@@ -192,30 +194,39 @@ def tile_full_tmix_params_pc_t_kernel(tc, y, r, k, v, g_hid, g2, r_k, ln_g, ln_b
                     f_t = work.tile([P, 4, P], F32)
                     nc.vector.tensor_tensor(out=f_t[:], in0=e_t[:], in1=w_ps[:], op=ALU.add)
                     nc.vector.tensor_tensor(
-                        out=grp[:, g],
+                        out=grp[:, j, g],
                         in0=f_t[:].rearrange("p t m -> p m t"),
                         in1=g_ps[:].rearrange("p t m -> p m t"),
                         op=ALU.mult,
                     )
 
-                z_codes = work.tile([P, NPASS * P], U32, align_bytes=64)
-                z_scales = work.tile([P, NPASS * P], U8, align_bytes=64)
-                nc.vector.quantize_mx(
-                    out=z_codes[:].bitcast(FP8X4),
-                    scales=z_scales[:],
-                    in_=grp[:].rearrange("p g m t -> p (g m t)"),
+            z_codes = big.tile([P, JMAX * NPASS * P], U32, align_bytes=64)
+            z_scales = big.tile([P, JMAX * NPASS * P], U8, align_bytes=64)
+            nw = nb * NPASS * P
+            nc.vector.quantize_mx(
+                out=z_codes[:, :nw].bitcast(FP8X4),
+                scales=z_scales[:, :nw],
+                in_=grp[:, :nb].rearrange("p j g m t -> p (j g m t)"),
+            )
+            o_sb = big.tile([P, JMAX * CO], F32)
+            for j0 in range(0, nb, 2):
+                npair = min(2, nb - j0)
+                o_ps = psum.tile([P, 2, CO], F32, bufs=1)
+                for u in range(npair):
+                    for g in range(NPASS):
+                        i0 = ((j0 + u) * NPASS + g) * P
+                        nc.tensor.matmul_mx(
+                            out=o_ps[:, u, :],
+                            lhsT=z_codes[:, i0 : i0 + P].bitcast(FP8X4),
+                            lhsT_scale=z_scales[:, i0 : i0 + P],
+                            rhs=w_codes[:, g * CO : (g + 1) * CO].bitcast(FP8X4),
+                            rhs_scale=w_scales[:, g * CO : (g + 1) * CO],
+                            start=(g == 0),
+                            stop=(g == NPASS - 1),
+                        )
+                nc.scalar.copy(
+                    out=o_sb[:, j0 * CO : (j0 + npair) * CO],
+                    in_=o_ps[:, :npair, :].rearrange("p u o -> p (u o)"),
                 )
-                o_ps = psum.tile([P, CO], F32, bufs=1)
-                for g in range(NPASS):
-                    nc.tensor.matmul_mx(
-                        out=o_ps[:],
-                        lhsT=z_codes[:, g * P : (g + 1) * P].bitcast(FP8X4),
-                        lhsT_scale=z_scales[:, g * P : (g + 1) * P],
-                        rhs=w_codes[:, g * CO : (g + 1) * CO].bitcast(FP8X4),
-                        rhs_scale=w_scales[:, g * CO : (g + 1) * CO],
-                        start=(g == 0),
-                        stop=(g == NPASS - 1),
-                    )
-                o_sb = work.tile([P, CO], F32)
-                nc.scalar.copy(out=o_sb[:], in_=o_ps[:])
-                nc.scalar.dma_start(out=out_v[s][:, j, :], in_=o_sb[:])
+            nc.scalar.dma_start(out=bview(out_f), in_=o_sb[:, : nb * CO])
+            t0 += P * nb

@@ -14,6 +14,7 @@ AX = mybir.AxisListType
 
 P = 128
 TOK = 4096
+NT = TOK // P
 C = 1024
 CO = 256
 HS = 64
@@ -22,46 +23,119 @@ DG = 128
 EPS_GN = 0.00064
 NPASS = C // 512
 JMAX = 4
-BATCHES = (1, 1, 2, 4, 4, 4, 4, 4, 4, 2, 1, 1)
+M_BATCHES = (1, 1, 2) + (4,) * 7
+Q_BATCHES = (4,) * 7 + (2, 1, 1)
+LD_Y, L_ST = 9, 6
+LD_RK, L_PQ, L_RD = 5, 3, 2
+LD_V = 3
+LD_GH, L_GH = 4, 2
 
 FLOPS = 2 * TOK * DG * C + 2 * TOK * C * CO
 
 
+def batch_maps(sizes):
+    first = []
+    where = {}
+    t = 0
+    for b, n in enumerate(sizes):
+        first.append(t)
+        for j in range(n):
+            where[t + j] = (b, j)
+        t += n
+    return first, where
+
+
 def tile_full_tmix_params_pc_t_kernel(tc, y, r, k, v, g_hid, g2, r_k, ln_g, ln_b, W_o, out):
     nc = tc.nc
-
     y_f = y.flatten_outer_dims()
     r_f = r.flatten_outer_dims()
     k_f = k.flatten_outer_dims()
     v_f = v.flatten_outer_dims()
     gh_f = g_hid.flatten_outer_dims()
     out_f = out.flatten_outer_dims()
+    m_first, m_where = batch_maps(M_BATCHES)
+    q_first, q_where = batch_maps(Q_BATCHES)
 
     with ExitStack() as ctx:
         const = ctx.enter_context(tc.tile_pool(name="const", bufs=1))
-        inp = ctx.enter_context(tc.tile_pool(name="inp", bufs=3))
+        ypool = ctx.enter_context(tc.tile_pool(name="ypool", bufs=LD_Y + 2))
+        rkpool = ctx.enter_context(tc.tile_pool(name="rkpool", bufs=LD_RK + 1))
+        vpool = ctx.enter_context(tc.tile_pool(name="vpool", bufs=LD_V + 2))
         work = ctx.enter_context(tc.tile_pool(name="work", bufs=3))
         big = ctx.enter_context(tc.tile_pool(name="big", bufs=2))
-        small = ctx.enter_context(tc.tile_pool(name="small", bufs=2))
+        stats = ctx.enter_context(tc.tile_pool(name="stats", bufs=5))
+        small = ctx.enter_context(tc.tile_pool(name="small", bufs=3))
         psum = ctx.enter_context(tc.psum_pool(name="psum", bufs=2))
 
-        ident_f = const.tile([P, P], F32)
-        make_identity(nc, ident_f[:])
-        ident_b = const.tile([P, P], BF16)
-        make_identity(nc, ident_b[:])
+        y_of, r_of, k_of, v_of, gh_of, ght_of, q_of, dot_of = {}, {}, {}, {}, {}, {}, {}, {}
+        st_of, rstd_of, shift_of, grp_of = {}, {}, {}, {}
 
+        def ld_y(t):
+            y_t = ypool.tile([P, C], BF16)
+            nc.sync.dma_start(out=y_t[:], in_=y_f[t * P : (t + 1) * P, :])
+            y_of[t] = y_t
+
+        def ld_rk(t):
+            r_t = rkpool.tile([P, C], BF16)
+            nc.sync.dma_start(out=r_t[:], in_=r_f[t * P : (t + 1) * P, :])
+            r_of[t] = r_t
+            k_t = rkpool.tile([P, C], BF16)
+            nc.sync.dma_start(out=k_t[:], in_=k_f[t * P : (t + 1) * P, :])
+            k_of[t] = k_t
+
+        def ld_v(t):
+            v_t = vpool.tile([P, C], BF16)
+            nc.sync.dma_start(out=v_t[:], in_=v_f[t * P : (t + 1) * P, :])
+            v_of[t] = v_t
+
+        def ld_gh(grp_i):
+            gh = small.tile([P, JMAX, DG], BF16)
+            nc.sync.dma_start(
+                out=gh[:],
+                in_=gh_f[grp_i * JMAX * P : (grp_i + 1) * JMAX * P, :].rearrange("(j p) d -> p j d", p=P),
+            )
+            gh_of[grp_i] = gh
+
+        rk_b = const.tile([P, C], BF16)
+        nc.scalar.dma_start(out=rk_b[:], in_=r_k.rearrange("h c -> (h c)").partition_broadcast(P))
         rows = const.tile([P, P], BF16)
         nc.gpsimd.memset(rows[:], 0.0)
         nc.scalar.dma_start(out=rows[0:8, :], in_=ln_g.rearrange("(a c) -> a c", c=P))
         nc.scalar.dma_start(out=rows[8:16, :], in_=ln_b.rearrange("(a c) -> a c", c=P))
         g2_sb = const.tile([P, C], BF16)
-        nc.scalar.dma_start(out=g2_sb[:], in_=g2)
         w_raw = const.tile([P, 2, C], BF16)
-        nc.scalar.dma_start(out=w_raw[:], in_=W_o.rearrange("(a p) c -> p a c", p=P))
-        rk_b = const.tile([P, C], BF16)
-        nc.scalar.dma_start(out=rk_b[:], in_=r_k.rearrange("h c -> (h c)").partition_broadcast(P))
+
+        ld_rk(0)
+        ld_y(0)
+        ld_y(1)
+        ld_y(2)
+        ld_rk(1)
+        ld_y(3)
+        ld_y(4)
+        ld_v(0)
+        ld_y(5)
+        ld_gh(0)
+        nc.sync.dma_start(out=g2_sb[:], in_=g2)
+        ld_y(6)
+        ld_rk(2)
+        ld_y(7)
+        ld_y(8)
+        ld_v(1)
+        nc.sync.dma_start(out=w_raw[:], in_=W_o.rearrange("(a p) c -> p a c", p=P))
+        ld_rk(3)
+        ld_v(2)
+        ld_rk(4)
+
+        ident_b = const.tile([P, P], BF16)
+        make_identity(nc, ident_b[:])
+        ident_f = const.tile([P, P], F32)
+        make_identity(nc, ident_f[:])
+        zero_t = const.tile([P, 1], F32)
+        nc.gpsimd.memset(zero_t[:], 0.0)
         eps_t = const.tile([P, 1], F32)
-        nc.gpsimd.memset(eps_t[:], EPS_GN)
+        nc.vector.tensor_scalar(
+            out=eps_t[:], in0=zero_t[:], scalar1=1.0, scalar2=EPS_GN, op0=ALU.mult, op1=ALU.add
+        )
 
         rows_t = psum.tile([P, P], BF16, tag="misc", bufs=1)
         nc.tensor.transpose(rows_t[:], rows[:], ident_b[:])
@@ -70,145 +144,149 @@ def tile_full_tmix_params_pc_t_kernel(tc, y, r, k, v, g_hid, g2, r_k, ln_g, ln_b
 
         w_codes = const.tile([P, NPASS * CO], U32, align_bytes=64)
         w_scales = const.tile([P, NPASS * CO], U8, align_bytes=64)
-        for g in range(NPASS):
-            w_t = psum.tile([P, 4, CO], BF16, tag="misc", bufs=1)
-            for t in range(4):
-                for a in range(2):
-                    cb = g * 4 + t
-                    nc.tensor.transpose(
-                        w_t[:, t, a * P : (a + 1) * P], w_raw[:, a, cb * P : (cb + 1) * P], ident_b[:]
-                    )
-            w_grp = const.tile([P, CO, 4], BF16, align_bytes=64)
-            nc.vector.tensor_copy(out=w_grp[:], in_=w_t[:].rearrange("p t o -> p o t"))
-            nc.vector.quantize_mx(
-                out=w_codes[:, g * CO : (g + 1) * CO].bitcast(FP8X4),
-                scales=w_scales[:, g * CO : (g + 1) * CO],
-                in_=w_grp[:].rearrange("p o t -> p (o t)"),
+
+        def prep_w():
+            for g in range(NPASS):
+                w_t = psum.tile([P, 4, CO], BF16, tag="misc", bufs=1)
+                for t in range(4):
+                    for a in range(2):
+                        cb = g * 4 + t
+                        nc.tensor.transpose(
+                            w_t[:, t, a * P : (a + 1) * P], w_raw[:, a, cb * P : (cb + 1) * P], ident_b[:]
+                        )
+                w_grp = const.tile([P, CO, 4], BF16, align_bytes=64)
+                nc.scalar.copy(out=w_grp[:], in_=w_t[:].rearrange("p t o -> p o t"))
+                nc.vector.quantize_mx(
+                    out=w_codes[:, g * CO : (g + 1) * CO].bitcast(FP8X4),
+                    scales=w_scales[:, g * CO : (g + 1) * CO],
+                    in_=w_grp[:].rearrange("p o t -> p (o t)"),
+                )
+
+        def pq(t):
+            q = work.tile([P, C], F32)
+            nc.gpsimd.tensor_tensor(out=q[:], in0=r_of[t][:], in1=k_of[t][:], op=ALU.mult)
+            nc.gpsimd.tensor_tensor(out=q[:], in0=q[:], in1=rk_b[:], op=ALU.mult)
+            q_of[t] = q
+
+        def rd(t):
+            dot = stats.tile([P, H], F32, bufs=6)
+            nc.vector.tensor_reduce(
+                out=dot[:], in_=q_of[t][:].rearrange("p (h c) -> p h c", c=HS), axis=AX.X, op=ALU.add
             )
+            dot_of[t] = dot
 
-        t0 = 0
-        for nb in BATCHES:
-            def bview(x):
-                return x[t0 : t0 + P * nb, :].rearrange("(p j) c -> p (j c)", j=nb)
-
-            r_t = inp.tile([P, JMAX * C], BF16)
-            nc.sync.dma_start(out=r_t[:, : nb * C], in_=bview(r_f))
-            k_t = inp.tile([P, JMAX * C], BF16)
-            nc.sync.dma_start(out=k_t[:, : nb * C], in_=bview(k_f))
-            y_t = inp.tile([P, JMAX * C], BF16)
-            nc.sync.dma_start(out=y_t[:, : nb * C], in_=bview(y_f))
-            v_t = inp.tile([P, JMAX * C], BF16)
-            nc.sync.dma_start(out=v_t[:, : nb * C], in_=bview(v_f))
-            gh = small.tile([P, JMAX * DG], BF16)
-            nc.sync.dma_start(out=gh[:, : nb * DG], in_=bview(gh_f))
-
-            gh_ps = psum.tile([P, JMAX, P], BF16, tag="misc", bufs=1)
-            for j in range(nb):
-                nc.tensor.transpose(gh_ps[:, j, :], gh[:, j * DG : (j + 1) * DG], ident_b[:])
-            gh_t = small.tile([P, JMAX, P], BF16)
-            nc.vector.tensor_copy(out=gh_t[:, :nb, :], in_=gh_ps[:, :nb, :])
-
-            nh = nb * H
-            st = small.tile([P, JMAX * H * 3], F32)
-            dot = small.tile([P, JMAX * H], F32)
-            for j in range(nb):
-                q = work.tile([P, C], F32)
+        def st_stage(t):
+            b, j = m_where[t]
+            if j == 0:
+                st = stats.tile([P, JMAX * H * 3], F32)
+                st_of[b] = st
+            st = st_of[b]
+            for hp in range(H // 2):
+                i0 = (j * (H // 2) + hp) * 6
+                nc.vector.bn_stats(
+                    out=st[:, i0 : i0 + 6],
+                    in_=y_of[t][:, hp * 2 * HS : (hp + 1) * 2 * HS].rearrange("p (h c) -> p c h", h=2),
+                )
+            if j == M_BATCHES[b] - 1:
+                nh = M_BATCHES[b] * H
+                st_v = st[:].rearrange("p (n t) -> p n t", t=3)
+                std = stats.tile([P, JMAX * H], F32)
+                nc.scalar.activation(
+                    out=std[:, :nh], in_=st_v[:, :nh, 2], func=ACTF.Sqrt, bias=eps_t[:, 0:1], scale=1.0 / HS
+                )
+                negmean = stats.tile([P, JMAX * H], F32)
+                nc.scalar.activation(out=negmean[:, :nh], in_=st_v[:, :nh, 1], func=ACTF.Copy, scale=-1.0)
+                rstd = stats.tile([P, JMAX * H], F32)
+                nc.vector.reciprocal(out=rstd[:, :nh], in_=std[:, :nh])
+                shift = stats.tile([P, JMAX * H], F32)
                 nc.gpsimd.tensor_tensor(
-                    out=q[:], in0=r_t[:, j * C : (j + 1) * C], in1=k_t[:, j * C : (j + 1) * C], op=ALU.mult
+                    out=shift[:, :nh], in0=negmean[:, :nh], in1=rstd[:, :nh], op=ALU.mult
                 )
-                nc.gpsimd.tensor_tensor(out=q[:], in0=q[:], in1=rk_b[:], op=ALU.mult)
-                for hp in range(H // 2):
-                    c0 = j * C + hp * 2 * HS
-                    i0 = (j * (H // 2) + hp) * 6
-                    nc.vector.bn_stats(
-                        out=st[:, i0 : i0 + 6],
-                        in_=y_t[:, c0 : c0 + 2 * HS].rearrange("p (h c) -> p c h", h=2),
+                rstd_of[b] = rstd
+                shift_of[b] = shift
+
+        def gh_stage(grp_i):
+            gh_ps = psum.tile([P, JMAX, P], BF16, tag="misc", bufs=1)
+            for j in range(JMAX):
+                nc.tensor.transpose(gh_ps[:, j, :], gh_of[grp_i][:, j, :], ident_b[:])
+            gh_t = small.tile([P, JMAX, P], BF16)
+            nc.scalar.copy(out=gh_t[:], in_=gh_ps[:])
+            ght_of[grp_i] = gh_t
+
+        def late(t):
+            mb, mj = m_where[t]
+            qb, qj = q_where[t]
+            rstd, shift, dot = rstd_of[mb], shift_of[mb], dot_of[t]
+            y_t, v_t = y_of[t], v_of[t]
+            if qj == 0:
+                grp = big.tile([P, JMAX, NPASS, P, 4], BF16, align_bytes=64)
+                grp_of[qb] = grp
+            grp = grp_of[qb]
+            n_t = work.tile([P, C], F32)
+            w_t2 = work.tile([P, C], F32)
+            for h in range(H):
+                col = mj * H + h
+                cs = slice(h * HS, (h + 1) * HS)
+                nc.scalar.activation(
+                    out=n_t[:, cs],
+                    in_=y_t[:, cs],
+                    func=ACTF.Identity,
+                    bias=shift[:, col : col + 1],
+                    scale=rstd[:, col : col + 1],
+                )
+                nc.scalar.activation(out=w_t2[:, cs], in_=v_t[:, cs], func=ACTF.Copy, scale=dot[:, h : h + 1])
+            for g in range(NPASS):
+                n_ps = psum.tile([P, 4, P], F32)
+                w_ps = psum.tile([P, 4, P], F32)
+                g_ps = psum.tile([P, 4, P], F32)
+                for u in range(4):
+                    cb = g * 4 + u
+                    nc.tensor.transpose(n_ps[:, u, :], n_t[:, cb * P : (cb + 1) * P], ident_f[:])
+                for u in range(4):
+                    cb = g * 4 + u
+                    nc.tensor.transpose(w_ps[:, u, :], w_t2[:, cb * P : (cb + 1) * P], ident_f[:])
+                for u in range(4):
+                    cb = g * 4 + u
+                    nc.tensor.matmul(
+                        g_ps[:, u, :],
+                        lhsT=g2_sb[:, cb * P : (cb + 1) * P],
+                        rhs=ght_of[t // JMAX][:, t % JMAX, :],
+                        start=True,
+                        stop=True,
                     )
-                nc.vector.tensor_reduce(
-                    out=dot[:, j * H : (j + 1) * H],
-                    in_=q[:].rearrange("p (h c) -> p h c", c=HS),
-                    axis=AX.X,
-                    op=ALU.add,
-                )
-
-            st_v = st[:].rearrange("p (n t) -> p n t", t=3)
-            std = small.tile([P, JMAX * H], F32)
-            nc.scalar.activation(
-                out=std[:, :nh], in_=st_v[:, :nh, 2], func=ACTF.Sqrt, bias=eps_t[:, 0:1], scale=1.0 / HS
-            )
-            negmean = small.tile([P, JMAX * H], F32)
-            nc.scalar.activation(out=negmean[:, :nh], in_=st_v[:, :nh, 1], func=ACTF.Copy, scale=-1.0)
-            rstd = small.tile([P, JMAX * H], F32)
-            nc.vector.reciprocal(out=rstd[:, :nh], in_=std[:, :nh])
-            shift = small.tile([P, JMAX * H], F32)
-            nc.gpsimd.tensor_tensor(out=shift[:, :nh], in0=negmean[:, :nh], in1=rstd[:, :nh], op=ALU.mult)
-
-            grp = big.tile([P, JMAX, NPASS, P, 4], BF16, align_bytes=64)
-            for j in range(nb):
-                n_t = work.tile([P, C], F32)
-                w_t2 = work.tile([P, C], F32)
-                for h in range(H):
-                    col = j * H + h
-                    src = slice(j * C + h * HS, j * C + (h + 1) * HS)
-                    dst = slice(h * HS, (h + 1) * HS)
+                e_t = work.tile([P, 4, P], F32)
+                for u in range(4):
+                    cb = g * 4 + u
                     nc.scalar.activation(
-                        out=n_t[:, dst],
-                        in_=y_t[:, src],
+                        out=e_t[:, u, :],
+                        in_=n_ps[:, u, :],
                         func=ACTF.Identity,
-                        bias=shift[:, col : col + 1],
-                        scale=rstd[:, col : col + 1],
+                        bias=lgb[:, 8 + cb : 9 + cb],
+                        scale=lgb[:, cb : cb + 1],
                     )
-                    nc.scalar.activation(
-                        out=w_t2[:, dst], in_=v_t[:, src], func=ACTF.Copy, scale=dot[:, col : col + 1]
-                    )
+                f_t = work.tile([P, 4, P], F32)
+                nc.vector.tensor_tensor(out=f_t[:], in0=e_t[:], in1=w_ps[:], op=ALU.add)
+                nc.vector.tensor_tensor(
+                    out=grp[:, qj, g],
+                    in0=f_t[:].rearrange("p u m -> p m u"),
+                    in1=g_ps[:].rearrange("p u m -> p m u"),
+                    op=ALU.mult,
+                )
+            if qj == Q_BATCHES[qb] - 1:
+                finish(qb)
 
-                for g in range(NPASS):
-                    n_ps = psum.tile([P, 4, P], F32)
-                    w_ps = psum.tile([P, 4, P], F32)
-                    g_ps = psum.tile([P, 4, P], F32)
-                    for t in range(4):
-                        cb = g * 4 + t
-                        nc.tensor.transpose(n_ps[:, t, :], n_t[:, cb * P : (cb + 1) * P], ident_f[:])
-                    for t in range(4):
-                        cb = g * 4 + t
-                        nc.tensor.transpose(w_ps[:, t, :], w_t2[:, cb * P : (cb + 1) * P], ident_f[:])
-                    for t in range(4):
-                        cb = g * 4 + t
-                        nc.tensor.matmul(
-                            g_ps[:, t, :],
-                            lhsT=g2_sb[:, cb * P : (cb + 1) * P],
-                            rhs=gh_t[:, j, :],
-                            start=True,
-                            stop=True,
-                        )
-                    e_t = work.tile([P, 4, P], F32)
-                    for t in range(4):
-                        cb = g * 4 + t
-                        nc.scalar.activation(
-                            out=e_t[:, t, :],
-                            in_=n_ps[:, t, :],
-                            func=ACTF.Identity,
-                            bias=lgb[:, 8 + cb : 9 + cb],
-                            scale=lgb[:, cb : cb + 1],
-                        )
-                    f_t = work.tile([P, 4, P], F32)
-                    nc.vector.tensor_tensor(out=f_t[:], in0=e_t[:], in1=w_ps[:], op=ALU.add)
-                    nc.vector.tensor_tensor(
-                        out=grp[:, j, g],
-                        in0=f_t[:].rearrange("p t m -> p m t"),
-                        in1=g_ps[:].rearrange("p t m -> p m t"),
-                        op=ALU.mult,
-                    )
-
+        def finish(qb):
+            nb = Q_BATCHES[qb]
+            grp = grp_of[qb]
             z_codes = big.tile([P, JMAX * NPASS * P], U32, align_bytes=64)
             z_scales = big.tile([P, JMAX * NPASS * P], U8, align_bytes=64)
             nw = nb * NPASS * P
             nc.vector.quantize_mx(
                 out=z_codes[:, :nw].bitcast(FP8X4),
                 scales=z_scales[:, :nw],
-                in_=grp[:, :nb].rearrange("p j g m t -> p (j g m t)"),
+                in_=grp[:, :nb].rearrange("p j g m u -> p (j g m u)"),
             )
-            o_sb = big.tile([P, JMAX * CO], F32)
+            o_sb = big.tile([P, JMAX, CO], F32)
             for j0 in range(0, nb, 2):
                 npair = min(2, nb - j0)
                 o_ps = psum.tile([P, 2, CO], F32, bufs=1)
@@ -224,9 +302,31 @@ def tile_full_tmix_params_pc_t_kernel(tc, y, r, k, v, g_hid, g2, r_k, ln_g, ln_b
                             start=(g == 0),
                             stop=(g == NPASS - 1),
                         )
-                nc.scalar.copy(
-                    out=o_sb[:, j0 * CO : (j0 + npair) * CO],
-                    in_=o_ps[:, :npair, :].rearrange("p u o -> p (u o)"),
-                )
-            nc.scalar.dma_start(out=bview(out_f), in_=o_sb[:, : nb * CO])
-            t0 += P * nb
+                nc.scalar.copy(out=o_sb[:, j0 : j0 + npair, :], in_=o_ps[:, :npair, :])
+            t0 = q_first[qb] * P
+            nc.scalar.dma_start(
+                out=out_f[t0 : t0 + nb * P, :].rearrange("(j p) o -> p j o", p=P), in_=o_sb[:, :nb, :]
+            )
+
+        for i in range(-L_ST, NT):
+            if i >= 0:
+                if i + LD_Y < NT:
+                    ld_y(i + LD_Y)
+                if i + LD_RK < NT:
+                    ld_rk(i + LD_RK)
+                if i + LD_V < NT:
+                    ld_v(i + LD_V)
+                if (i + LD_GH) % JMAX == 0 and i + LD_GH < NT:
+                    ld_gh((i + LD_GH) // JMAX)
+            if 0 <= i + L_PQ < NT:
+                pq(i + L_PQ)
+            if 0 <= i + L_ST < NT:
+                st_stage(i + L_ST)
+            if 0 <= i + L_RD < NT:
+                rd(i + L_RD)
+            if (i + L_GH) % JMAX == 0 and 0 <= i + L_GH < NT:
+                gh_stage((i + L_GH) // JMAX)
+            if i == -1:
+                prep_w()
+            if i >= 0:
+                late(i)

@@ -26,8 +26,9 @@ JMAX = 4
 M_BATCHES = (1, 1, 2) + (4,) * 7
 Q_BATCHES = (4,) * 7 + (2, 1, 1)
 LD_Y, L_ST = 9, 6
-LD_RK, L_PQ, L_RD = 5, 3, 2
-LD_V = 3
+LD_RK, L_PQ, L_DOT, L_W = 8, 6, 5, 3
+LD_V = 5
+ACT_W_EVERY = 4
 LD_GH, L_GH = 4, 2
 
 FLOPS = 2 * TOK * DG * C + 2 * TOK * C * CO
@@ -62,12 +63,13 @@ def tile_full_tmix_params_pc_t_kernel(tc, y, r, k, v, g_hid, g2, r_k, ln_g, ln_b
         rkpool = ctx.enter_context(tc.tile_pool(name="rkpool", bufs=LD_RK + 1))
         vpool = ctx.enter_context(tc.tile_pool(name="vpool", bufs=LD_V + 2))
         work = ctx.enter_context(tc.tile_pool(name="work", bufs=3))
+        wpool = ctx.enter_context(tc.tile_pool(name="wpool", bufs=L_W + 2))
         big = ctx.enter_context(tc.tile_pool(name="big", bufs=2))
         stats = ctx.enter_context(tc.tile_pool(name="stats", bufs=5))
         small = ctx.enter_context(tc.tile_pool(name="small", bufs=3))
         psum = ctx.enter_context(tc.psum_pool(name="psum", bufs=2))
 
-        y_of, r_of, k_of, v_of, gh_of, ght_of, q_of, dot_of = {}, {}, {}, {}, {}, {}, {}, {}
+        y_of, r_of, k_of, v_of, gh_of, ght_of, q_of, dot_of, w_of = {}, {}, {}, {}, {}, {}, {}, {}, {}
         st_of, rstd_of, shift_of, grp_of = {}, {}, {}, {}
 
         def ld_y(t):
@@ -96,35 +98,39 @@ def tile_full_tmix_params_pc_t_kernel(tc, y, r, k, v, g_hid, g2, r_k, ln_g, ln_b
             )
             gh_of[grp_i] = gh
 
-        rk_b = const.tile([P, C], BF16)
-        nc.scalar.dma_start(out=rk_b[:], in_=r_k.rearrange("h c -> (h c)").partition_broadcast(P))
         rows = const.tile([P, P], BF16)
         nc.gpsimd.memset(rows[:], 0.0)
         nc.scalar.dma_start(out=rows[0:8, :], in_=ln_g.rearrange("(a c) -> a c", c=P))
         nc.scalar.dma_start(out=rows[8:16, :], in_=ln_b.rearrange("(a c) -> a c", c=P))
+        nc.scalar.dma_start(out=rows[16:24, :], in_=r_k.rearrange("(a b) c -> a (b c)", b=2))
         g2_sb = const.tile([P, C], BF16)
         w_raw = const.tile([P, 2, C], BF16)
 
         ld_rk(0)
         ld_y(0)
+        ld_rk(1)
         ld_y(1)
         ld_y(2)
-        ld_rk(1)
+        ld_rk(2)
         ld_y(3)
-        ld_y(4)
         ld_v(0)
-        ld_y(5)
+        ld_rk(3)
+        ld_y(4)
         ld_gh(0)
         nc.sync.dma_start(out=g2_sb[:], in_=g2)
-        ld_y(6)
-        ld_rk(2)
-        ld_y(7)
-        ld_y(8)
-        ld_v(1)
-        nc.sync.dma_start(out=w_raw[:], in_=W_o.rearrange("(a p) c -> p a c", p=P))
-        ld_rk(3)
-        ld_v(2)
+        ld_y(5)
         ld_rk(4)
+        ld_v(1)
+        ld_y(6)
+        ld_rk(5)
+        ld_y(7)
+        nc.sync.dma_start(out=w_raw[:], in_=W_o.rearrange("(a p) c -> p a c", p=P))
+        ld_v(2)
+        ld_rk(6)
+        ld_y(8)
+        ld_rk(7)
+        ld_v(3)
+        ld_v(4)
 
         ident_b = const.tile([P, P], BF16)
         make_identity(nc, ident_b[:])
@@ -141,6 +147,21 @@ def tile_full_tmix_params_pc_t_kernel(tc, y, r, k, v, g_hid, g2, r_k, ln_g, ln_b
         nc.tensor.transpose(rows_t[:], rows[:], ident_b[:])
         lgb = const.tile([P, 16], F32)
         nc.vector.tensor_copy(out=lgb[:], in_=rows_t[:, 0:16])
+        half_mask = const.tile([P, 2], F32)
+        nc.vector.tensor_reduce(
+            out=half_mask[:], in_=ident_f[:].rearrange("p (a b) -> p a b", a=2), axis=AX.X, op=ALU.add
+        )
+        ind = const.tile([P, 8 * 18], F32)
+        nc.gpsimd.memset(ind[:], 0.0)
+        ind_v = ind[:].rearrange("p (a b) -> p a b", b=18)
+        for hh in range(2):
+            nc.vector.tensor_scalar(
+                out=ind_v[:, :, hh],
+                in0=rows_t[:, 16:24],
+                scalar1=half_mask[:, hh : hh + 1],
+                scalar2=None,
+                op0=ALU.mult,
+            )
 
         w_codes = const.tile([P, NPASS * CO], U32, align_bytes=64)
         w_scales = const.tile([P, NPASS * CO], U8, align_bytes=64)
@@ -165,15 +186,48 @@ def tile_full_tmix_params_pc_t_kernel(tc, y, r, k, v, g_hid, g2, r_k, ln_g, ln_b
         def pq(t):
             q = work.tile([P, C], F32)
             nc.gpsimd.tensor_tensor(out=q[:], in0=r_of[t][:], in1=k_of[t][:], op=ALU.mult)
-            nc.gpsimd.tensor_tensor(out=q[:], in0=q[:], in1=rk_b[:], op=ALU.mult)
             q_of[t] = q
 
-        def rd(t):
-            dot = stats.tile([P, H], F32, bufs=6)
-            nc.vector.tensor_reduce(
-                out=dot[:], in_=q_of[t][:].rearrange("p (h c) -> p h c", c=HS), axis=AX.X, op=ALU.add
-            )
+        def dot_stage(t):
+            q_t = work.tile([P, 8, P], F32)
+            for g in range(NPASS):
+                q_ps = psum.tile([P, 4, P], F32, bufs=1)
+                for u in range(4):
+                    cb = g * 4 + u
+                    nc.tensor.transpose(q_ps[:, u, :], q_of[t][:, cb * P : (cb + 1) * P], ident_f[:])
+                if g == 0:
+                    nc.scalar.copy(out=q_t[:, 0:4, :], in_=q_ps[:])
+                else:
+                    nc.vector.tensor_copy(out=q_t[:, 4:8, :], in_=q_ps[:])
+            d_ps = psum.tile([P, H], F32, tag="misc", bufs=1)
+            for cb in range(8):
+                nc.tensor.matmul(
+                    d_ps[:],
+                    lhsT=q_t[:, cb, :],
+                    rhs=ind[:, cb * H : (cb + 1) * H],
+                    start=(cb == 0),
+                    stop=(cb == 7),
+                )
+            dot = stats.tile([P, H], F32, bufs=8)
+            nc.vector.tensor_copy(out=dot[:], in_=d_ps[:])
             dot_of[t] = dot
+
+        def w_stage(t):
+            w_t2 = wpool.tile([P, C], F32)
+            w_of[t] = w_t2
+            if t % ACT_W_EVERY == ACT_W_EVERY - 1:
+                for h in range(H):
+                    cs = slice(h * HS, (h + 1) * HS)
+                    nc.scalar.activation(
+                        out=w_t2[:, cs], in_=v_of[t][:, cs], func=ACTF.Copy, scale=dot_of[t][:, h : h + 1]
+                    )
+            else:
+                nc.gpsimd.tensor_tensor(
+                    out=w_t2[:].rearrange("p (h c) -> p h c", c=HS),
+                    in0=v_of[t][:].rearrange("p (h c) -> p h c", c=HS),
+                    in1=dot_of[t][:].unsqueeze(2).to_broadcast([P, H, HS]),
+                    op=ALU.mult,
+                )
 
         def st_stage(t):
             b, j = m_where[t]
@@ -216,14 +270,13 @@ def tile_full_tmix_params_pc_t_kernel(tc, y, r, k, v, g_hid, g2, r_k, ln_g, ln_b
         def late(t):
             mb, mj = m_where[t]
             qb, qj = q_where[t]
-            rstd, shift, dot = rstd_of[mb], shift_of[mb], dot_of[t]
-            y_t, v_t = y_of[t], v_of[t]
+            rstd, shift = rstd_of[mb], shift_of[mb]
+            y_t, w_t2 = y_of[t], w_of[t]
             if qj == 0:
                 grp = big.tile([P, JMAX, NPASS, P, 4], BF16, align_bytes=64)
                 grp_of[qb] = grp
             grp = grp_of[qb]
             n_t = work.tile([P, C], F32)
-            w_t2 = work.tile([P, C], F32)
             for h in range(H):
                 col = mj * H + h
                 cs = slice(h * HS, (h + 1) * HS)
@@ -234,7 +287,6 @@ def tile_full_tmix_params_pc_t_kernel(tc, y, r, k, v, g_hid, g2, r_k, ln_g, ln_b
                     bias=shift[:, col : col + 1],
                     scale=rstd[:, col : col + 1],
                 )
-                nc.scalar.activation(out=w_t2[:, cs], in_=v_t[:, cs], func=ACTF.Copy, scale=dot[:, h : h + 1])
             for g in range(NPASS):
                 n_ps = psum.tile([P, 4, P], F32)
                 w_ps = psum.tile([P, 4, P], F32)
@@ -289,7 +341,7 @@ def tile_full_tmix_params_pc_t_kernel(tc, y, r, k, v, g_hid, g2, r_k, ln_g, ln_b
             o_sb = big.tile([P, JMAX, CO], F32)
             for j0 in range(0, nb, 2):
                 npair = min(2, nb - j0)
-                o_ps = psum.tile([P, 2, CO], F32, bufs=1)
+                o_ps = psum.tile([P, 2, CO], F32, tag="misc", bufs=1)
                 for u in range(npair):
                     for g in range(NPASS):
                         i0 = ((j0 + u) * NPASS + g) * P
@@ -322,8 +374,10 @@ def tile_full_tmix_params_pc_t_kernel(tc, y, r, k, v, g_hid, g2, r_k, ln_g, ln_b
                 pq(i + L_PQ)
             if 0 <= i + L_ST < NT:
                 st_stage(i + L_ST)
-            if 0 <= i + L_RD < NT:
-                rd(i + L_RD)
+            if 0 <= i + L_DOT < NT:
+                dot_stage(i + L_DOT)
+            if 0 <= i + L_W < NT:
+                w_stage(i + L_W)
             if (i + L_GH) % JMAX == 0 and 0 <= i + L_GH < NT:
                 gh_stage((i + L_GH) // JMAX)
             if i == -1:

@@ -26,9 +26,8 @@ JMAX = 4
 M_BATCHES = (1, 1, 2) + (4,) * 7
 Q_BATCHES = (4,) * 7 + (2, 1, 1)
 LD_Y, L_ST = 9, 6
-LD_RK, L_PQ, L_DOT, L_W = 8, 6, 5, 3
-LD_V = 5
-ACT_W_EVERY = 4
+LD_RK, L_PQ, L_RD = 5, 3, 2
+LD_V = 3
 LD_GH, L_GH = 4, 2
 
 FLOPS = 2 * TOK * DG * C + 2 * TOK * C * CO
@@ -63,13 +62,12 @@ def tile_full_tmix_params_pc_t_kernel(tc, y, r, k, v, g_hid, g2, r_k, ln_g, ln_b
         rkpool = ctx.enter_context(tc.tile_pool(name="rkpool", bufs=LD_RK + 1))
         vpool = ctx.enter_context(tc.tile_pool(name="vpool", bufs=LD_V + 2))
         work = ctx.enter_context(tc.tile_pool(name="work", bufs=3))
-        wpool = ctx.enter_context(tc.tile_pool(name="wpool", bufs=L_W + 2))
         big = ctx.enter_context(tc.tile_pool(name="big", bufs=2))
         stats = ctx.enter_context(tc.tile_pool(name="stats", bufs=5))
         small = ctx.enter_context(tc.tile_pool(name="small", bufs=3))
         psum = ctx.enter_context(tc.psum_pool(name="psum", bufs=2))
 
-        y_of, r_of, k_of, v_of, gh_of, ght_of, q_of, dot_of, w_of = {}, {}, {}, {}, {}, {}, {}, {}, {}
+        y_of, r_of, k_of, v_of, gh_of, ght_of, q_of, dot_of = {}, {}, {}, {}, {}, {}, {}, {}
         st_of, rstd_of, shift_of, grp_of = {}, {}, {}, {}
 
         def ld_y(t):
@@ -98,39 +96,35 @@ def tile_full_tmix_params_pc_t_kernel(tc, y, r, k, v, g_hid, g2, r_k, ln_g, ln_b
             )
             gh_of[grp_i] = gh
 
+        rk_b = const.tile([P, C], BF16)
+        nc.scalar.dma_start(out=rk_b[:], in_=r_k.rearrange("h c -> (h c)").partition_broadcast(P))
         rows = const.tile([P, P], BF16)
         nc.gpsimd.memset(rows[:], 0.0)
         nc.scalar.dma_start(out=rows[0:8, :], in_=ln_g.rearrange("(a c) -> a c", c=P))
         nc.scalar.dma_start(out=rows[8:16, :], in_=ln_b.rearrange("(a c) -> a c", c=P))
-        nc.scalar.dma_start(out=rows[16:24, :], in_=r_k.rearrange("(a b) c -> a (b c)", b=2))
         g2_sb = const.tile([P, C], BF16)
         w_raw = const.tile([P, 2, C], BF16)
 
         ld_rk(0)
         ld_y(0)
-        ld_rk(1)
         ld_y(1)
         ld_y(2)
-        ld_rk(2)
+        ld_rk(1)
         ld_y(3)
-        ld_v(0)
-        ld_rk(3)
         ld_y(4)
+        ld_v(0)
+        ld_y(5)
         ld_gh(0)
         nc.sync.dma_start(out=g2_sb[:], in_=g2)
-        ld_y(5)
-        ld_rk(4)
-        ld_v(1)
         ld_y(6)
-        ld_rk(5)
+        ld_rk(2)
         ld_y(7)
-        nc.sync.dma_start(out=w_raw[:], in_=W_o.rearrange("(a p) c -> p a c", p=P))
-        ld_v(2)
-        ld_rk(6)
         ld_y(8)
-        ld_rk(7)
-        ld_v(3)
-        ld_v(4)
+        ld_v(1)
+        nc.sync.dma_start(out=w_raw[:], in_=W_o.rearrange("(a p) c -> p a c", p=P))
+        ld_rk(3)
+        ld_v(2)
+        ld_rk(4)
 
         ident_b = const.tile([P, P], BF16)
         make_identity(nc, ident_b[:])
@@ -147,21 +141,6 @@ def tile_full_tmix_params_pc_t_kernel(tc, y, r, k, v, g_hid, g2, r_k, ln_g, ln_b
         nc.tensor.transpose(rows_t[:], rows[:], ident_b[:])
         lgb = const.tile([P, 16], F32)
         nc.vector.tensor_copy(out=lgb[:], in_=rows_t[:, 0:16])
-        half_mask = const.tile([P, 2], F32)
-        nc.vector.tensor_reduce(
-            out=half_mask[:], in_=ident_f[:].rearrange("p (a b) -> p a b", a=2), axis=AX.X, op=ALU.add
-        )
-        ind = const.tile([P, 8 * 18], F32)
-        nc.gpsimd.memset(ind[:], 0.0)
-        ind_v = ind[:].rearrange("p (a b) -> p a b", b=18)
-        for hh in range(2):
-            nc.vector.tensor_scalar(
-                out=ind_v[:, :, hh],
-                in0=rows_t[:, 16:24],
-                scalar1=half_mask[:, hh : hh + 1],
-                scalar2=None,
-                op0=ALU.mult,
-            )
 
         w_codes = const.tile([P, NPASS * CO], U32, align_bytes=64)
         w_scales = const.tile([P, NPASS * CO], U8, align_bytes=64)
@@ -186,48 +165,15 @@ def tile_full_tmix_params_pc_t_kernel(tc, y, r, k, v, g_hid, g2, r_k, ln_g, ln_b
         def pq(t):
             q = work.tile([P, C], F32)
             nc.gpsimd.tensor_tensor(out=q[:], in0=r_of[t][:], in1=k_of[t][:], op=ALU.mult)
+            nc.gpsimd.tensor_tensor(out=q[:], in0=q[:], in1=rk_b[:], op=ALU.mult)
             q_of[t] = q
 
-        def dot_stage(t):
-            q_t = work.tile([P, 8, P], F32)
-            for g in range(NPASS):
-                q_ps = psum.tile([P, 4, P], F32, bufs=1)
-                for u in range(4):
-                    cb = g * 4 + u
-                    nc.tensor.transpose(q_ps[:, u, :], q_of[t][:, cb * P : (cb + 1) * P], ident_f[:])
-                if g == 0:
-                    nc.scalar.copy(out=q_t[:, 0:4, :], in_=q_ps[:])
-                else:
-                    nc.vector.tensor_copy(out=q_t[:, 4:8, :], in_=q_ps[:])
-            d_ps = psum.tile([P, H], F32, tag="misc", bufs=1)
-            for cb in range(8):
-                nc.tensor.matmul(
-                    d_ps[:],
-                    lhsT=q_t[:, cb, :],
-                    rhs=ind[:, cb * H : (cb + 1) * H],
-                    start=(cb == 0),
-                    stop=(cb == 7),
-                )
-            dot = stats.tile([P, H], F32, bufs=8)
-            nc.vector.tensor_copy(out=dot[:], in_=d_ps[:])
+        def rd(t):
+            dot = stats.tile([P, H], F32, bufs=6)
+            nc.vector.tensor_reduce(
+                out=dot[:], in_=q_of[t][:].rearrange("p (h c) -> p h c", c=HS), axis=AX.X, op=ALU.add
+            )
             dot_of[t] = dot
-
-        def w_stage(t):
-            w_t2 = wpool.tile([P, C], F32)
-            w_of[t] = w_t2
-            if t % ACT_W_EVERY == ACT_W_EVERY - 1:
-                for h in range(H):
-                    cs = slice(h * HS, (h + 1) * HS)
-                    nc.scalar.activation(
-                        out=w_t2[:, cs], in_=v_of[t][:, cs], func=ACTF.Copy, scale=dot_of[t][:, h : h + 1]
-                    )
-            else:
-                nc.gpsimd.tensor_tensor(
-                    out=w_t2[:].rearrange("p (h c) -> p h c", c=HS),
-                    in0=v_of[t][:].rearrange("p (h c) -> p h c", c=HS),
-                    in1=dot_of[t][:].unsqueeze(2).to_broadcast([P, H, HS]),
-                    op=ALU.mult,
-                )
 
         def st_stage(t):
             b, j = m_where[t]
@@ -244,14 +190,16 @@ def tile_full_tmix_params_pc_t_kernel(tc, y, r, k, v, g_hid, g2, r_k, ln_g, ln_b
             if j == M_BATCHES[b] - 1:
                 nh = M_BATCHES[b] * H
                 st_v = st[:].rearrange("p (n t) -> p n t", t=3)
-                std = stats.tile([P, JMAX * H], F32)
+                rstd = stats.tile([P, JMAX * H], F32)
                 nc.scalar.activation(
-                    out=std[:, :nh], in_=st_v[:, :nh, 2], func=ACTF.Sqrt, bias=eps_t[:, 0:1], scale=1.0 / HS
+                    out=rstd[:, :nh],
+                    in_=st_v[:, :nh, 2],
+                    func=ACTF.Abs_reciprocal_sqrt,
+                    bias=eps_t[:, 0:1],
+                    scale=1.0 / HS,
                 )
                 negmean = stats.tile([P, JMAX * H], F32)
                 nc.scalar.activation(out=negmean[:, :nh], in_=st_v[:, :nh, 1], func=ACTF.Copy, scale=-1.0)
-                rstd = stats.tile([P, JMAX * H], F32)
-                nc.vector.reciprocal(out=rstd[:, :nh], in_=std[:, :nh])
                 shift = stats.tile([P, JMAX * H], F32)
                 nc.gpsimd.tensor_tensor(
                     out=shift[:, :nh], in0=negmean[:, :nh], in1=rstd[:, :nh], op=ALU.mult
@@ -270,13 +218,14 @@ def tile_full_tmix_params_pc_t_kernel(tc, y, r, k, v, g_hid, g2, r_k, ln_g, ln_b
         def late(t):
             mb, mj = m_where[t]
             qb, qj = q_where[t]
-            rstd, shift = rstd_of[mb], shift_of[mb]
-            y_t, w_t2 = y_of[t], w_of[t]
+            rstd, shift, dot = rstd_of[mb], shift_of[mb], dot_of[t]
+            y_t, v_t = y_of[t], v_of[t]
             if qj == 0:
                 grp = big.tile([P, JMAX, NPASS, P, 4], BF16, align_bytes=64)
                 grp_of[qb] = grp
             grp = grp_of[qb]
             n_t = work.tile([P, C], F32)
+            w_t2 = work.tile([P, C], F32)
             for h in range(H):
                 col = mj * H + h
                 cs = slice(h * HS, (h + 1) * HS)
@@ -287,6 +236,7 @@ def tile_full_tmix_params_pc_t_kernel(tc, y, r, k, v, g_hid, g2, r_k, ln_g, ln_b
                     bias=shift[:, col : col + 1],
                     scale=rstd[:, col : col + 1],
                 )
+                nc.scalar.activation(out=w_t2[:, cs], in_=v_t[:, cs], func=ACTF.Copy, scale=dot[:, h : h + 1])
             for g in range(NPASS):
                 n_ps = psum.tile([P, 4, P], F32)
                 w_ps = psum.tile([P, 4, P], F32)
@@ -341,7 +291,7 @@ def tile_full_tmix_params_pc_t_kernel(tc, y, r, k, v, g_hid, g2, r_k, ln_g, ln_b
             o_sb = big.tile([P, JMAX, CO], F32)
             for j0 in range(0, nb, 2):
                 npair = min(2, nb - j0)
-                o_ps = psum.tile([P, 2, CO], F32, tag="misc", bufs=1)
+                o_ps = psum.tile([P, 2, CO], F32, bufs=1)
                 for u in range(npair):
                     for g in range(NPASS):
                         i0 = ((j0 + u) * NPASS + g) * P
@@ -374,10 +324,8 @@ def tile_full_tmix_params_pc_t_kernel(tc, y, r, k, v, g_hid, g2, r_k, ln_g, ln_b
                 pq(i + L_PQ)
             if 0 <= i + L_ST < NT:
                 st_stage(i + L_ST)
-            if 0 <= i + L_DOT < NT:
-                dot_stage(i + L_DOT)
-            if 0 <= i + L_W < NT:
-                w_stage(i + L_W)
+            if 0 <= i + L_RD < NT:
+                rd(i + L_RD)
             if (i + L_GH) % JMAX == 0 and 0 <= i + L_GH < NT:
                 gh_stage((i + L_GH) // JMAX)
             if i == -1:

@@ -137,7 +137,7 @@ def tile_full_tmix_params_pc_t_kernel(tc, y, r, k, v, g_hid, g2, r_k, ln_g, ln_b
             out=eps_t[:], in0=zero_t[:], scalar1=1.0, scalar2=EPS_GN, op0=ALU.mult, op1=ALU.add
         )
 
-        rows_t = psum.tile([P, P], BF16, tag="misc", bufs=1)
+        rows_t = psum.tile([P, P], BF16, tag="a", bufs=2)
         nc.tensor.transpose(rows_t[:], rows[:], ident_b[:])
         lgb = const.tile([P, 16], F32)
         nc.vector.tensor_copy(out=lgb[:], in_=rows_t[:, 0:16])
@@ -147,7 +147,7 @@ def tile_full_tmix_params_pc_t_kernel(tc, y, r, k, v, g_hid, g2, r_k, ln_g, ln_b
 
         def prep_w():
             for g in range(NPASS):
-                w_t = psum.tile([P, 4, CO], BF16, tag="misc", bufs=1)
+                w_t = psum.tile([P, 4, CO], BF16, tag="a", bufs=2)
                 for t in range(4):
                     for a in range(2):
                         cb = g * 4 + t
@@ -190,16 +190,14 @@ def tile_full_tmix_params_pc_t_kernel(tc, y, r, k, v, g_hid, g2, r_k, ln_g, ln_b
             if j == M_BATCHES[b] - 1:
                 nh = M_BATCHES[b] * H
                 st_v = st[:].rearrange("p (n t) -> p n t", t=3)
-                rstd = stats.tile([P, JMAX * H], F32)
+                std = stats.tile([P, JMAX * H], F32)
                 nc.scalar.activation(
-                    out=rstd[:, :nh],
-                    in_=st_v[:, :nh, 2],
-                    func=ACTF.Abs_reciprocal_sqrt,
-                    bias=eps_t[:, 0:1],
-                    scale=1.0 / HS,
+                    out=std[:, :nh], in_=st_v[:, :nh, 2], func=ACTF.Sqrt, bias=eps_t[:, 0:1], scale=1.0 / HS
                 )
                 negmean = stats.tile([P, JMAX * H], F32)
                 nc.scalar.activation(out=negmean[:, :nh], in_=st_v[:, :nh, 1], func=ACTF.Copy, scale=-1.0)
+                rstd = stats.tile([P, JMAX * H], F32)
+                nc.vector.reciprocal(out=rstd[:, :nh], in_=std[:, :nh])
                 shift = stats.tile([P, JMAX * H], F32)
                 nc.gpsimd.tensor_tensor(
                     out=shift[:, :nh], in0=negmean[:, :nh], in1=rstd[:, :nh], op=ALU.mult
@@ -208,7 +206,7 @@ def tile_full_tmix_params_pc_t_kernel(tc, y, r, k, v, g_hid, g2, r_k, ln_g, ln_b
                 shift_of[b] = shift
 
         def gh_stage(grp_i):
-            gh_ps = psum.tile([P, JMAX, P], BF16, tag="misc", bufs=1)
+            gh_ps = psum.tile([P, JMAX, P], BF16, tag="a", bufs=2)
             for j in range(JMAX):
                 nc.tensor.transpose(gh_ps[:, j, :], gh_of[grp_i][:, j, :], ident_b[:])
             gh_t = small.tile([P, JMAX, P], BF16)
@@ -238,9 +236,9 @@ def tile_full_tmix_params_pc_t_kernel(tc, y, r, k, v, g_hid, g2, r_k, ln_g, ln_b
                 )
                 nc.scalar.activation(out=w_t2[:, cs], in_=v_t[:, cs], func=ACTF.Copy, scale=dot[:, h : h + 1])
             for g in range(NPASS):
-                n_ps = psum.tile([P, 4, P], F32)
-                w_ps = psum.tile([P, 4, P], F32)
-                g_ps = psum.tile([P, 4, P], F32)
+                n_ps = psum.tile([P, 4, P], F32, tag="a", bufs=2)
+                w_ps = psum.tile([P, 4, P], F32, bufs=3)
+                g_ps = psum.tile([P, 4, P], F32, bufs=3)
                 for u in range(4):
                     cb = g * 4 + u
                     nc.tensor.transpose(n_ps[:, u, :], n_t[:, cb * P : (cb + 1) * P], ident_f[:])
@@ -291,7 +289,7 @@ def tile_full_tmix_params_pc_t_kernel(tc, y, r, k, v, g_hid, g2, r_k, ln_g, ln_b
             o_sb = big.tile([P, JMAX, CO], F32)
             for j0 in range(0, nb, 2):
                 npair = min(2, nb - j0)
-                o_ps = psum.tile([P, 2, CO], F32, bufs=1)
+                o_ps = psum.tile([P, 2, CO], F32, tag="a", bufs=2)
                 for u in range(npair):
                     for g in range(NPASS):
                         i0 = ((j0 + u) * NPASS + g) * P

@@ -13,24 +13,30 @@ ACTF = mybir.ActivationFunctionType
 AX = mybir.AxisListType
 
 P = 128
-TOK = 4096
-NT = TOK // P
+TOKENS = 4096
+NT = TOKENS // P
 C = 1024
 CO = 256
 HS = 64
 H = C // HS
 DG = 128
 EPS_GN = 0.00064
-NPASS = C // 512
-JMAX = 4
-M_BATCHES = (1, 1, 2) + (4,) * 7
-Q_BATCHES = (4,) * 7 + (2, 1, 1)
-LD_Y, L_ST = 9, 6
-LD_RK, L_PQ, L_RD = 5, 3, 2
-LD_V = 3
-LD_GH, L_GH = 4, 2
+PACK = 4
+NPASS = C // (P * PACK)
+NBLK = C // P
+GROUP = 4
 
-FLOPS = 2 * TOK * DG * C + 2 * TOK * C * CO
+NORM_BATCHES = (1, 1, 2) + (GROUP,) * 7
+MX_BATCHES = (GROUP,) * 7 + (2, 1, 1)
+
+LOAD_AHEAD = 8
+STATS_AHEAD = 6
+PRODUCT_AHEAD = 3
+DOT_AHEAD = 2
+GATE_LOAD_AHEAD = 4
+GATE_AHEAD = 2
+
+FLOPS = 2 * TOKENS * DG * C + 2 * TOKENS * C * CO
 
 
 def batch_maps(sizes):
@@ -53,78 +59,52 @@ def tile_full_tmix_params_pc_t_kernel(tc, y, r, k, v, g_hid, g2, r_k, ln_g, ln_b
     v_f = v.flatten_outer_dims()
     gh_f = g_hid.flatten_outer_dims()
     out_f = out.flatten_outer_dims()
-    m_first, m_where = batch_maps(M_BATCHES)
-    q_first, q_where = batch_maps(Q_BATCHES)
+    norm_where = batch_maps(NORM_BATCHES)[1]
+    mx_first, mx_where = batch_maps(MX_BATCHES)
 
     with ExitStack() as ctx:
         const = ctx.enter_context(tc.tile_pool(name="const", bufs=1))
-        ypool = ctx.enter_context(tc.tile_pool(name="ypool", bufs=LD_Y + 2))
-        rkpool = ctx.enter_context(tc.tile_pool(name="rkpool", bufs=LD_RK + 1))
-        vpool = ctx.enter_context(tc.tile_pool(name="vpool", bufs=LD_V + 2))
+        inputs = ctx.enter_context(tc.tile_pool(name="inputs", bufs=LOAD_AHEAD + 2))
         work = ctx.enter_context(tc.tile_pool(name="work", bufs=3))
-        big = ctx.enter_context(tc.tile_pool(name="big", bufs=2))
+        batch = ctx.enter_context(tc.tile_pool(name="batch", bufs=2))
         stats = ctx.enter_context(tc.tile_pool(name="stats", bufs=5))
-        small = ctx.enter_context(tc.tile_pool(name="small", bufs=3))
+        gate = ctx.enter_context(tc.tile_pool(name="gate", bufs=3))
         psum = ctx.enter_context(tc.psum_pool(name="psum", bufs=2))
 
         y_of, r_of, k_of, v_of, gh_of, ght_of, q_of, dot_of = {}, {}, {}, {}, {}, {}, {}, {}
-        st_of, rstd_of, shift_of, grp_of = {}, {}, {}, {}
+        st_of, rstd_of, shift_of, z_of = {}, {}, {}, {}
 
-        def ld_y(t):
-            y_t = ypool.tile([P, C], BF16)
-            nc.sync.dma_start(out=y_t[:], in_=y_f[t * P : (t + 1) * P, :])
-            y_of[t] = y_t
-
-        def ld_rk(t):
-            r_t = rkpool.tile([P, C], BF16)
-            nc.sync.dma_start(out=r_t[:], in_=r_f[t * P : (t + 1) * P, :])
+        def load_tile(t):
+            rows = slice(t * P, (t + 1) * P)
+            r_t = inputs.tile([P, C], BF16)
+            nc.sync.dma_start(out=r_t[:], in_=r_f[rows, :])
             r_of[t] = r_t
-            k_t = rkpool.tile([P, C], BF16)
-            nc.sync.dma_start(out=k_t[:], in_=k_f[t * P : (t + 1) * P, :])
+            k_t = inputs.tile([P, C], BF16)
+            nc.sync.dma_start(out=k_t[:], in_=k_f[rows, :])
             k_of[t] = k_t
-
-        def ld_v(t):
-            v_t = vpool.tile([P, C], BF16)
-            nc.sync.dma_start(out=v_t[:], in_=v_f[t * P : (t + 1) * P, :])
+            y_t = inputs.tile([P, C], BF16)
+            nc.sync.dma_start(out=y_t[:], in_=y_f[rows, :])
+            y_of[t] = y_t
+            v_t = inputs.tile([P, C], BF16)
+            nc.sync.dma_start(out=v_t[:], in_=v_f[rows, :])
             v_of[t] = v_t
 
-        def ld_gh(grp_i):
-            gh = small.tile([P, JMAX, DG], BF16)
+        def load_gate_hidden(grp):
+            gh = gate.tile([P, GROUP, DG], BF16)
             nc.sync.dma_start(
                 out=gh[:],
-                in_=gh_f[grp_i * JMAX * P : (grp_i + 1) * JMAX * P, :].rearrange("(j p) d -> p j d", p=P),
+                in_=gh_f[grp * GROUP * P : (grp + 1) * GROUP * P, :].rearrange("(j p) d -> p j d", p=P),
             )
-            gh_of[grp_i] = gh
+            gh_of[grp] = gh
 
         rk_b = const.tile([P, C], BF16)
         nc.scalar.dma_start(out=rk_b[:], in_=r_k.rearrange("h c -> (h c)").partition_broadcast(P))
-        rows = const.tile([P, P], BF16)
-        nc.gpsimd.memset(rows[:], 0.0)
-        nc.scalar.dma_start(out=rows[0:8, :], in_=ln_g.rearrange("(a c) -> a c", c=P))
-        nc.scalar.dma_start(out=rows[8:16, :], in_=ln_b.rearrange("(a c) -> a c", c=P))
+        ln_rows = const.tile([P, P], BF16)
+        nc.gpsimd.memset(ln_rows[:], 0.0)
+        nc.scalar.dma_start(out=ln_rows[0:NBLK, :], in_=ln_g.rearrange("(a c) -> a c", c=P))
+        nc.scalar.dma_start(out=ln_rows[NBLK : 2 * NBLK, :], in_=ln_b.rearrange("(a c) -> a c", c=P))
         g2_sb = const.tile([P, C], BF16)
-        w_raw = const.tile([P, 2, C], BF16)
-
-        ld_rk(0)
-        ld_y(0)
-        ld_y(1)
-        ld_y(2)
-        ld_rk(1)
-        ld_y(3)
-        ld_y(4)
-        ld_v(0)
-        ld_y(5)
-        ld_gh(0)
-        nc.sync.dma_start(out=g2_sb[:], in_=g2)
-        ld_y(6)
-        ld_rk(2)
-        ld_y(7)
-        ld_y(8)
-        ld_v(1)
-        nc.sync.dma_start(out=w_raw[:], in_=W_o.rearrange("(a p) c -> p a c", p=P))
-        ld_rk(3)
-        ld_v(2)
-        ld_rk(4)
+        w_raw = const.tile([P, CO // P, C], BF16)
 
         ident_b = const.tile([P, P], BF16)
         make_identity(nc, ident_b[:])
@@ -137,164 +117,164 @@ def tile_full_tmix_params_pc_t_kernel(tc, y, r, k, v, g_hid, g2, r_k, ln_g, ln_b
             out=eps_t[:], in0=zero_t[:], scalar1=1.0, scalar2=EPS_GN, op0=ALU.mult, op1=ALU.add
         )
 
-        rows_t = psum.tile([P, P], BF16, tag="a", bufs=2)
-        nc.tensor.transpose(rows_t[:], rows[:], ident_b[:])
-        lgb = const.tile([P, 16], F32)
-        nc.vector.tensor_copy(out=lgb[:], in_=rows_t[:, 0:16])
+        ln_ps = psum.tile([P, P], BF16, tag="setup", bufs=1)
+        nc.tensor.transpose(ln_ps[:], ln_rows[:], ident_b[:])
+        ln_cols = const.tile([P, 2 * NBLK], F32)
+        nc.vector.tensor_copy(out=ln_cols[:], in_=ln_ps[:, 0 : 2 * NBLK])
 
         w_codes = const.tile([P, NPASS * CO], U32, align_bytes=64)
         w_scales = const.tile([P, NPASS * CO], U8, align_bytes=64)
 
-        def prep_w():
+        def quantise_weights():
             for g in range(NPASS):
-                w_t = psum.tile([P, 4, CO], BF16, tag="a", bufs=2)
-                for t in range(4):
-                    for a in range(2):
-                        cb = g * 4 + t
+                wt_ps = psum.tile([P, PACK, CO], BF16, tag="setup", bufs=1)
+                for u in range(PACK):
+                    blk = g * PACK + u
+                    for a in range(CO // P):
                         nc.tensor.transpose(
-                            w_t[:, t, a * P : (a + 1) * P], w_raw[:, a, cb * P : (cb + 1) * P], ident_b[:]
+                            wt_ps[:, u, a * P : (a + 1) * P], w_raw[:, a, blk * P : (blk + 1) * P], ident_b[:]
                         )
-                w_grp = const.tile([P, CO, 4], BF16, align_bytes=64)
-                nc.scalar.copy(out=w_grp[:], in_=w_t[:].rearrange("p t o -> p o t"))
+                w_bf = const.tile([P, CO, PACK], BF16, align_bytes=64)
+                nc.scalar.copy(out=w_bf[:], in_=wt_ps[:].rearrange("p u o -> p o u"))
                 nc.vector.quantize_mx(
                     out=w_codes[:, g * CO : (g + 1) * CO].bitcast(FP8X4),
                     scales=w_scales[:, g * CO : (g + 1) * CO],
-                    in_=w_grp[:].rearrange("p o t -> p (o t)"),
+                    in_=w_bf[:].rearrange("p o u -> p (o u)"),
                 )
 
-        def pq(t):
+        def bonus_products(t):
             q = work.tile([P, C], F32)
             nc.gpsimd.tensor_tensor(out=q[:], in0=r_of[t][:], in1=k_of[t][:], op=ALU.mult)
             nc.gpsimd.tensor_tensor(out=q[:], in0=q[:], in1=rk_b[:], op=ALU.mult)
             q_of[t] = q
 
-        def rd(t):
-            dot = stats.tile([P, H], F32, bufs=6)
+        def bonus_dot(t):
+            dot = stats.tile([P, H], F32)
             nc.vector.tensor_reduce(
                 out=dot[:], in_=q_of[t][:].rearrange("p (h c) -> p h c", c=HS), axis=AX.X, op=ALU.add
             )
             dot_of[t] = dot
 
-        def st_stage(t):
-            b, j = m_where[t]
+        def norm_stats(t):
+            b, j = norm_where[t]
             if j == 0:
-                st = stats.tile([P, JMAX * H * 3], F32)
+                st = stats.tile([P, GROUP * H * 3], F32)
                 st_of[b] = st
             st = st_of[b]
-            for hp in range(H // 2):
-                i0 = (j * (H // 2) + hp) * 6
+            for a in range(H // 2):
+                i0 = (j * (H // 2) + a) * 6
                 nc.vector.bn_stats(
                     out=st[:, i0 : i0 + 6],
-                    in_=y_of[t][:, hp * 2 * HS : (hp + 1) * 2 * HS].rearrange("p (h c) -> p c h", h=2),
+                    in_=y_of[t][:, a * 2 * HS : (a + 1) * 2 * HS].rearrange("p (h c) -> p c h", h=2),
                 )
-            if j == M_BATCHES[b] - 1:
-                nh = M_BATCHES[b] * H
-                st_v = st[:].rearrange("p (n t) -> p n t", t=3)
-                std = stats.tile([P, JMAX * H], F32)
+            if j == NORM_BATCHES[b] - 1:
+                nh = NORM_BATCHES[b] * H
+                st_v = st[:].rearrange("p (n s) -> p n s", s=3)
+                std = stats.tile([P, GROUP * H], F32)
                 nc.scalar.activation(
                     out=std[:, :nh], in_=st_v[:, :nh, 2], func=ACTF.Sqrt, bias=eps_t[:, 0:1], scale=1.0 / HS
                 )
-                negmean = stats.tile([P, JMAX * H], F32)
+                negmean = stats.tile([P, GROUP * H], F32)
                 nc.scalar.activation(out=negmean[:, :nh], in_=st_v[:, :nh, 1], func=ACTF.Copy, scale=-1.0)
-                rstd = stats.tile([P, JMAX * H], F32)
+                rstd = stats.tile([P, GROUP * H], F32)
                 nc.vector.reciprocal(out=rstd[:, :nh], in_=std[:, :nh])
-                shift = stats.tile([P, JMAX * H], F32)
+                shift = stats.tile([P, GROUP * H], F32)
                 nc.gpsimd.tensor_tensor(
                     out=shift[:, :nh], in0=negmean[:, :nh], in1=rstd[:, :nh], op=ALU.mult
                 )
                 rstd_of[b] = rstd
                 shift_of[b] = shift
 
-        def gh_stage(grp_i):
-            gh_ps = psum.tile([P, JMAX, P], BF16, tag="a", bufs=2)
-            for j in range(JMAX):
-                nc.tensor.transpose(gh_ps[:, j, :], gh_of[grp_i][:, j, :], ident_b[:])
-            gh_t = small.tile([P, JMAX, P], BF16)
+        def transpose_gate_hidden(grp):
+            gh_ps = psum.tile([P, GROUP, P], BF16, tag="setup", bufs=1)
+            for j in range(GROUP):
+                nc.tensor.transpose(gh_ps[:, j, :], gh_of[grp][:, j, :], ident_b[:])
+            gh_t = gate.tile([P, GROUP, P], BF16)
             nc.scalar.copy(out=gh_t[:], in_=gh_ps[:])
-            ght_of[grp_i] = gh_t
+            ght_of[grp] = gh_t
 
-        def late(t):
-            mb, mj = m_where[t]
-            qb, qj = q_where[t]
-            rstd, shift, dot = rstd_of[mb], shift_of[mb], dot_of[t]
-            y_t, v_t = y_of[t], v_of[t]
-            if qj == 0:
-                grp = big.tile([P, JMAX, NPASS, P, 4], BF16, align_bytes=64)
-                grp_of[qb] = grp
-            grp = grp_of[qb]
-            n_t = work.tile([P, C], F32)
-            w_t2 = work.tile([P, C], F32)
+        def finish_tile(t):
+            nb, nj = norm_where[t]
+            mb, mj = mx_where[t]
+            rstd, shift, dot = rstd_of[nb], shift_of[nb], dot_of[t]
+            if mj == 0:
+                z_bf = batch.tile([P, GROUP, NPASS, P, PACK], BF16, align_bytes=64)
+                z_of[mb] = z_bf
+            z_bf = z_of[mb]
+            normed = work.tile([P, C], F32)
+            bonus = work.tile([P, C], F32)
             for h in range(H):
-                col = mj * H + h
+                col = nj * H + h
                 cs = slice(h * HS, (h + 1) * HS)
                 nc.scalar.activation(
-                    out=n_t[:, cs],
-                    in_=y_t[:, cs],
+                    out=normed[:, cs],
+                    in_=y_of[t][:, cs],
                     func=ACTF.Identity,
                     bias=shift[:, col : col + 1],
                     scale=rstd[:, col : col + 1],
                 )
-                nc.scalar.activation(out=w_t2[:, cs], in_=v_t[:, cs], func=ACTF.Copy, scale=dot[:, h : h + 1])
+                nc.scalar.activation(
+                    out=bonus[:, cs], in_=v_of[t][:, cs], func=ACTF.Copy, scale=dot[:, h : h + 1]
+                )
             for g in range(NPASS):
-                n_ps = psum.tile([P, 4, P], F32, tag="a", bufs=2)
-                w_ps = psum.tile([P, 4, P], F32, bufs=3)
-                g_ps = psum.tile([P, 4, P], F32, bufs=3)
-                for u in range(4):
-                    cb = g * 4 + u
-                    nc.tensor.transpose(n_ps[:, u, :], n_t[:, cb * P : (cb + 1) * P], ident_f[:])
-                for u in range(4):
-                    cb = g * 4 + u
-                    nc.tensor.transpose(w_ps[:, u, :], w_t2[:, cb * P : (cb + 1) * P], ident_f[:])
-                for u in range(4):
-                    cb = g * 4 + u
+                normed_ps = psum.tile([P, PACK, P], F32)
+                bonus_ps = psum.tile([P, PACK, P], F32)
+                g_ps = psum.tile([P, PACK, P], F32)
+                for u in range(PACK):
+                    blk = g * PACK + u
+                    nc.tensor.transpose(normed_ps[:, u, :], normed[:, blk * P : (blk + 1) * P], ident_f[:])
+                for u in range(PACK):
+                    blk = g * PACK + u
+                    nc.tensor.transpose(bonus_ps[:, u, :], bonus[:, blk * P : (blk + 1) * P], ident_f[:])
+                for u in range(PACK):
+                    blk = g * PACK + u
                     nc.tensor.matmul(
                         g_ps[:, u, :],
-                        lhsT=g2_sb[:, cb * P : (cb + 1) * P],
-                        rhs=ght_of[t // JMAX][:, t % JMAX, :],
+                        lhsT=g2_sb[:, blk * P : (blk + 1) * P],
+                        rhs=ght_of[t // GROUP][:, t % GROUP, :],
                         start=True,
                         stop=True,
                     )
-                e_t = work.tile([P, 4, P], F32)
-                for u in range(4):
-                    cb = g * 4 + u
+                affine = work.tile([P, PACK, P], F32)
+                for u in range(PACK):
+                    blk = g * PACK + u
                     nc.scalar.activation(
-                        out=e_t[:, u, :],
-                        in_=n_ps[:, u, :],
+                        out=affine[:, u, :],
+                        in_=normed_ps[:, u, :],
                         func=ACTF.Identity,
-                        bias=lgb[:, 8 + cb : 9 + cb],
-                        scale=lgb[:, cb : cb + 1],
+                        bias=ln_cols[:, NBLK + blk : NBLK + blk + 1],
+                        scale=ln_cols[:, blk : blk + 1],
                     )
-                f_t = work.tile([P, 4, P], F32)
-                nc.vector.tensor_tensor(out=f_t[:], in0=e_t[:], in1=w_ps[:], op=ALU.add)
+                y2 = work.tile([P, PACK, P], F32)
+                nc.vector.tensor_tensor(out=y2[:], in0=affine[:], in1=bonus_ps[:], op=ALU.add)
                 nc.vector.tensor_tensor(
-                    out=grp[:, qj, g],
-                    in0=f_t[:].rearrange("p u m -> p m u"),
+                    out=z_bf[:, mj, g],
+                    in0=y2[:].rearrange("p u m -> p m u"),
                     in1=g_ps[:].rearrange("p u m -> p m u"),
                     op=ALU.mult,
                 )
-            if qj == Q_BATCHES[qb] - 1:
-                finish(qb)
+            if mj == MX_BATCHES[mb] - 1:
+                project(mb)
 
-        def finish(qb):
-            nb = Q_BATCHES[qb]
-            grp = grp_of[qb]
-            z_codes = big.tile([P, JMAX * NPASS * P], U32, align_bytes=64)
-            z_scales = big.tile([P, JMAX * NPASS * P], U8, align_bytes=64)
-            nw = nb * NPASS * P
+        def project(mb):
+            n_tiles = MX_BATCHES[mb]
+            words = n_tiles * NPASS * P
+            z_codes = batch.tile([P, GROUP * NPASS * P], U32, align_bytes=64)
+            z_scales = batch.tile([P, GROUP * NPASS * P], U8, align_bytes=64)
             nc.vector.quantize_mx(
-                out=z_codes[:, :nw].bitcast(FP8X4),
-                scales=z_scales[:, :nw],
-                in_=grp[:, :nb].rearrange("p j g m u -> p (j g m u)"),
+                out=z_codes[:, :words].bitcast(FP8X4),
+                scales=z_scales[:, :words],
+                in_=z_of[mb][:, :n_tiles].rearrange("p j g m u -> p (j g m u)"),
             )
-            o_sb = big.tile([P, JMAX, CO], F32)
-            for j0 in range(0, nb, 2):
-                npair = min(2, nb - j0)
-                o_ps = psum.tile([P, 2, CO], F32, tag="a", bufs=2)
-                for u in range(npair):
+            o_sb = batch.tile([P, GROUP, CO], F32)
+            for j0 in range(0, n_tiles, 2):
+                pair = min(2, n_tiles - j0)
+                o_ps = psum.tile([P, 2, CO], F32, bufs=1)
+                for a in range(pair):
                     for g in range(NPASS):
-                        i0 = ((j0 + u) * NPASS + g) * P
+                        i0 = ((j0 + a) * NPASS + g) * P
                         nc.tensor.matmul_mx(
-                            out=o_ps[:, u, :],
+                            out=o_ps[:, a, :],
                             lhsT=z_codes[:, i0 : i0 + P].bitcast(FP8X4),
                             lhsT_scale=z_scales[:, i0 : i0 + P],
                             rhs=w_codes[:, g * CO : (g + 1) * CO].bitcast(FP8X4),
@@ -302,31 +282,29 @@ def tile_full_tmix_params_pc_t_kernel(tc, y, r, k, v, g_hid, g2, r_k, ln_g, ln_b
                             start=(g == 0),
                             stop=(g == NPASS - 1),
                         )
-                nc.scalar.copy(out=o_sb[:, j0 : j0 + npair, :], in_=o_ps[:, :npair, :])
-            t0 = q_first[qb] * P
+                nc.scalar.copy(out=o_sb[:, j0 : j0 + pair, :], in_=o_ps[:, :pair, :])
+            t0 = mx_first[mb] * P
             nc.scalar.dma_start(
-                out=out_f[t0 : t0 + nb * P, :].rearrange("(j p) o -> p j o", p=P), in_=o_sb[:, :nb, :]
+                out=out_f[t0 : t0 + n_tiles * P, :].rearrange("(j p) o -> p j o", p=P), in_=o_sb[:, :n_tiles, :]
             )
 
-        for i in range(-L_ST, NT):
-            if i >= 0:
-                if i + LD_Y < NT:
-                    ld_y(i + LD_Y)
-                if i + LD_RK < NT:
-                    ld_rk(i + LD_RK)
-                if i + LD_V < NT:
-                    ld_v(i + LD_V)
-                if (i + LD_GH) % JMAX == 0 and i + LD_GH < NT:
-                    ld_gh((i + LD_GH) // JMAX)
-            if 0 <= i + L_PQ < NT:
-                pq(i + L_PQ)
-            if 0 <= i + L_ST < NT:
-                st_stage(i + L_ST)
-            if 0 <= i + L_RD < NT:
-                rd(i + L_RD)
-            if (i + L_GH) % JMAX == 0 and 0 <= i + L_GH < NT:
-                gh_stage((i + L_GH) // JMAX)
-            if i == -1:
-                prep_w()
-            if i >= 0:
-                late(i)
+        for slot in range(-LOAD_AHEAD, NT):
+            if slot + LOAD_AHEAD < NT:
+                load_tile(slot + LOAD_AHEAD)
+            if slot == 2 - LOAD_AHEAD:
+                nc.sync.dma_start(out=g2_sb[:], in_=g2)
+                nc.sync.dma_start(out=w_raw[:], in_=W_o.rearrange("(a p) c -> p a c", p=P))
+            if (slot + GATE_LOAD_AHEAD) % GROUP == 0 and 0 <= slot + GATE_LOAD_AHEAD < NT:
+                load_gate_hidden((slot + GATE_LOAD_AHEAD) // GROUP)
+            if 0 <= slot + PRODUCT_AHEAD < NT:
+                bonus_products(slot + PRODUCT_AHEAD)
+            if 0 <= slot + STATS_AHEAD < NT:
+                norm_stats(slot + STATS_AHEAD)
+            if 0 <= slot + DOT_AHEAD < NT:
+                bonus_dot(slot + DOT_AHEAD)
+            if (slot + GATE_AHEAD) % GROUP == 0 and 0 <= slot + GATE_AHEAD < NT:
+                transpose_gate_hidden((slot + GATE_AHEAD) // GROUP)
+            if slot == -1:
+                quantise_weights()
+            if slot >= 0:
+                finish_tile(slot)

@@ -29,7 +29,9 @@ GROUP = 4
 NORM_BATCHES = (1, 1, 2) + (GROUP,) * 7
 MX_BATCHES = (GROUP,) * 7 + (2, 1, 1)
 
-LOAD_AHEAD = 8
+Y_AHEAD = 10
+RK_AHEAD = 5
+V_AHEAD = 4
 STATS_AHEAD = 6
 PRODUCT_AHEAD = 3
 DOT_AHEAD = 2
@@ -64,7 +66,9 @@ def tile_full_tmix_params_pc_t_kernel(tc, y, r, k, v, g_hid, g2, r_k, ln_g, ln_b
 
     with ExitStack() as ctx:
         const = ctx.enter_context(tc.tile_pool(name="const", bufs=1))
-        inputs = ctx.enter_context(tc.tile_pool(name="inputs", bufs=LOAD_AHEAD + 2))
+        y_pool = ctx.enter_context(tc.tile_pool(name="y_pool", bufs=Y_AHEAD + 2))
+        rk_pool = ctx.enter_context(tc.tile_pool(name="rk_pool", bufs=RK_AHEAD + 1))
+        v_pool = ctx.enter_context(tc.tile_pool(name="v_pool", bufs=V_AHEAD + 2))
         work = ctx.enter_context(tc.tile_pool(name="work", bufs=3))
         batch = ctx.enter_context(tc.tile_pool(name="batch", bufs=2))
         stats = ctx.enter_context(tc.tile_pool(name="stats", bufs=5))
@@ -74,19 +78,22 @@ def tile_full_tmix_params_pc_t_kernel(tc, y, r, k, v, g_hid, g2, r_k, ln_g, ln_b
         y_of, r_of, k_of, v_of, gh_of, ght_of, q_of, dot_of = {}, {}, {}, {}, {}, {}, {}, {}
         st_of, rstd_of, shift_of, z_of = {}, {}, {}, {}
 
-        def load_tile(t):
-            rows = slice(t * P, (t + 1) * P)
-            r_t = inputs.tile([P, C], BF16)
-            nc.sync.dma_start(out=r_t[:], in_=r_f[rows, :])
+        def load_rk(t):
+            r_t = rk_pool.tile([P, C], BF16)
+            nc.sync.dma_start(out=r_t[:], in_=r_f[t * P : (t + 1) * P, :])
             r_of[t] = r_t
-            k_t = inputs.tile([P, C], BF16)
-            nc.sync.dma_start(out=k_t[:], in_=k_f[rows, :])
+            k_t = rk_pool.tile([P, C], BF16)
+            nc.sync.dma_start(out=k_t[:], in_=k_f[t * P : (t + 1) * P, :])
             k_of[t] = k_t
-            y_t = inputs.tile([P, C], BF16)
-            nc.sync.dma_start(out=y_t[:], in_=y_f[rows, :])
+
+        def load_y(t):
+            y_t = y_pool.tile([P, C], BF16)
+            nc.sync.dma_start(out=y_t[:], in_=y_f[t * P : (t + 1) * P, :])
             y_of[t] = y_t
-            v_t = inputs.tile([P, C], BF16)
-            nc.sync.dma_start(out=v_t[:], in_=v_f[rows, :])
+
+        def load_v(t):
+            v_t = v_pool.tile([P, C], BF16)
+            nc.sync.dma_start(out=v_t[:], in_=v_f[t * P : (t + 1) * P, :])
             v_of[t] = v_t
 
         def load_gate_hidden(grp):
@@ -105,6 +112,18 @@ def tile_full_tmix_params_pc_t_kernel(tc, y, r, k, v, g_hid, g2, r_k, ln_g, ln_b
         nc.scalar.dma_start(out=ln_rows[NBLK : 2 * NBLK, :], in_=ln_b.rearrange("(a c) -> a c", c=P))
         g2_sb = const.tile([P, C], BF16)
         w_raw = const.tile([P, CO // P, C], BF16)
+
+        for t in range(RK_AHEAD):
+            load_rk(t)
+            load_y(2 * t)
+            load_y(2 * t + 1)
+            if t >= 1:
+                load_v(t - 1)
+            if t == 1:
+                load_gate_hidden(0)
+                nc.sync.dma_start(out=g2_sb[:], in_=g2)
+            if t == 3:
+                nc.sync.dma_start(out=w_raw[:], in_=W_o.rearrange("(a p) c -> p a c", p=P))
 
         ident_b = const.tile([P, P], BF16)
         make_identity(nc, ident_b[:])
@@ -288,14 +307,16 @@ def tile_full_tmix_params_pc_t_kernel(tc, y, r, k, v, g_hid, g2, r_k, ln_g, ln_b
                 out=out_f[t0 : t0 + n_tiles * P, :].rearrange("(j p) o -> p j o", p=P), in_=o_sb[:, :n_tiles, :]
             )
 
-        for slot in range(-LOAD_AHEAD, NT):
-            if slot + LOAD_AHEAD < NT:
-                load_tile(slot + LOAD_AHEAD)
-            if slot == 2 - LOAD_AHEAD:
-                nc.sync.dma_start(out=g2_sb[:], in_=g2)
-                nc.sync.dma_start(out=w_raw[:], in_=W_o.rearrange("(a p) c -> p a c", p=P))
-            if (slot + GATE_LOAD_AHEAD) % GROUP == 0 and 0 <= slot + GATE_LOAD_AHEAD < NT:
-                load_gate_hidden((slot + GATE_LOAD_AHEAD) // GROUP)
+        for slot in range(-STATS_AHEAD, NT):
+            if slot >= 0:
+                if slot + Y_AHEAD < NT:
+                    load_y(slot + Y_AHEAD)
+                if slot + RK_AHEAD < NT:
+                    load_rk(slot + RK_AHEAD)
+                if slot + V_AHEAD < NT:
+                    load_v(slot + V_AHEAD)
+                if slot % GROUP == 0 and slot + GATE_LOAD_AHEAD < NT:
+                    load_gate_hidden((slot + GATE_LOAD_AHEAD) // GROUP)
             if 0 <= slot + PRODUCT_AHEAD < NT:
                 bonus_products(slot + PRODUCT_AHEAD)
             if 0 <= slot + STATS_AHEAD < NT:

from contextlib import ExitStack

import concourse.mybir as mybir
from concourse.masks import make_identity

F32 = mybir.dt.float32
BF16 = mybir.dt.bfloat16
U32 = mybir.dt.uint32
U8 = mybir.dt.uint8
FP8X4 = mybir.dt.float8_e4m3fn_x4
ALU = mybir.AluOpType
ACTF = mybir.ActivationFunctionType
AX = mybir.AxisListType

P = 128
TOKENS = 4096
NT = TOKENS // P
C = 1024
CO = 256
HS = 64
H = C // HS
DG = 128
EPS_GN = 0.00064
PACK = 4
NPASS = C // (P * PACK)
NBLK = C // P
GROUP = 4

NORM_BATCHES = (1, 1, 2) + (GROUP,) * 7
MX_BATCHES = (GROUP,) * 7 + (2, 1, 1)

Y_AHEAD = 10
RK_AHEAD = 5
V_AHEAD = 4
STATS_AHEAD = 6
PRODUCT_AHEAD = 3
DOT_AHEAD = 2
GATE_LOAD_AHEAD = 4
GATE_AHEAD = 2

FLOPS = 2 * TOKENS * DG * C + 2 * TOKENS * C * CO


def batch_maps(sizes):
    first = []
    where = {}
    t = 0
    for b, n in enumerate(sizes):
        first.append(t)
        for j in range(n):
            where[t + j] = (b, j)
        t += n
    return first, where


def tile_full_tmix_params_pc_t_kernel(tc, y, r, k, v, g_hid, g2, r_k, ln_g, ln_b, W_o, out):
    nc = tc.nc
    y_f = y.flatten_outer_dims()
    r_f = r.flatten_outer_dims()
    k_f = k.flatten_outer_dims()
    v_f = v.flatten_outer_dims()
    gh_f = g_hid.flatten_outer_dims()
    out_f = out.flatten_outer_dims()
    norm_where = batch_maps(NORM_BATCHES)[1]
    mx_first, mx_where = batch_maps(MX_BATCHES)

    with ExitStack() as ctx:
        const = ctx.enter_context(tc.tile_pool(name="const", bufs=1))
        y_pool = ctx.enter_context(tc.tile_pool(name="y_pool", bufs=Y_AHEAD + 2))
        rk_pool = ctx.enter_context(tc.tile_pool(name="rk_pool", bufs=RK_AHEAD + 1))
        v_pool = ctx.enter_context(tc.tile_pool(name="v_pool", bufs=V_AHEAD + 2))
        work = ctx.enter_context(tc.tile_pool(name="work", bufs=3))
        batch = ctx.enter_context(tc.tile_pool(name="batch", bufs=2))
        stats = ctx.enter_context(tc.tile_pool(name="stats", bufs=5))
        gate = ctx.enter_context(tc.tile_pool(name="gate", bufs=3))
        psum = ctx.enter_context(tc.psum_pool(name="psum", bufs=2))

        y_of, r_of, k_of, v_of, gh_of, ght_of, q_of, dot_of = {}, {}, {}, {}, {}, {}, {}, {}
        st_of, rstd_of, shift_of, z_of = {}, {}, {}, {}

        def load_rk(t):
            r_t = rk_pool.tile([P, C], BF16)
            nc.sync.dma_start(out=r_t[:], in_=r_f[t * P : (t + 1) * P, :])
            r_of[t] = r_t
            k_t = rk_pool.tile([P, C], BF16)
            nc.sync.dma_start(out=k_t[:], in_=k_f[t * P : (t + 1) * P, :])
            k_of[t] = k_t

        def load_y(t):
            y_t = y_pool.tile([P, C], BF16)
            nc.sync.dma_start(out=y_t[:], in_=y_f[t * P : (t + 1) * P, :])
            y_of[t] = y_t

        def load_v(t):
            v_t = v_pool.tile([P, C], BF16)
            nc.sync.dma_start(out=v_t[:], in_=v_f[t * P : (t + 1) * P, :])
            v_of[t] = v_t

        def load_gate_hidden(grp):
            gh = gate.tile([P, GROUP, DG], BF16)
            nc.sync.dma_start(
                out=gh[:],
                in_=gh_f[grp * GROUP * P : (grp + 1) * GROUP * P, :].rearrange("(j p) d -> p j d", p=P),
            )
            gh_of[grp] = gh

        rk_b = const.tile([P, C], BF16)
        nc.scalar.dma_start(out=rk_b[:], in_=r_k.rearrange("h c -> (h c)").partition_broadcast(P))
        ln_rows = const.tile([P, P], BF16)
        nc.gpsimd.memset(ln_rows[:], 0.0)
        nc.scalar.dma_start(out=ln_rows[0:NBLK, :], in_=ln_g.rearrange("(a c) -> a c", c=P))
        nc.scalar.dma_start(out=ln_rows[NBLK : 2 * NBLK, :], in_=ln_b.rearrange("(a c) -> a c", c=P))
        g2_sb = const.tile([P, C], BF16)
        w_raw = const.tile([P, CO // P, C], BF16)

        for t in range(RK_AHEAD):
            load_rk(t)
            load_y(2 * t)
            load_y(2 * t + 1)
            if t >= 1:
                load_v(t - 1)
            if t == 1:
                load_gate_hidden(0)
                nc.sync.dma_start(out=g2_sb[:], in_=g2)
            if t == 3:
                nc.sync.dma_start(out=w_raw[:], in_=W_o.rearrange("(a p) c -> p a c", p=P))

        ident_b = const.tile([P, P], BF16)
        make_identity(nc, ident_b[:])
        ident_f = const.tile([P, P], F32)
        make_identity(nc, ident_f[:])
        zero_t = const.tile([P, 1], F32)
        nc.gpsimd.memset(zero_t[:], 0.0)
        eps_t = const.tile([P, 1], F32)
        nc.vector.tensor_scalar(
            out=eps_t[:], in0=zero_t[:], scalar1=1.0, scalar2=EPS_GN, op0=ALU.mult, op1=ALU.add
        )

        ln_ps = psum.tile([P, P], BF16, tag="setup", bufs=1)
        nc.tensor.transpose(ln_ps[:], ln_rows[:], ident_b[:])
        ln_cols = const.tile([P, 2 * NBLK], F32)
        nc.vector.tensor_copy(out=ln_cols[:], in_=ln_ps[:, 0 : 2 * NBLK])

        w_codes = const.tile([P, NPASS * CO], U32, align_bytes=64)
        w_scales = const.tile([P, NPASS * CO], U8, align_bytes=64)

        def quantise_weights():
            for g in range(NPASS):
                wt_ps = psum.tile([P, PACK, CO], BF16, tag="setup", bufs=1)
                for u in range(PACK):
                    blk = g * PACK + u
                    for a in range(CO // P):
                        nc.tensor.transpose(
                            wt_ps[:, u, a * P : (a + 1) * P], w_raw[:, a, blk * P : (blk + 1) * P], ident_b[:]
                        )
                w_bf = const.tile([P, CO, PACK], BF16, align_bytes=64)
                nc.scalar.copy(out=w_bf[:], in_=wt_ps[:].rearrange("p u o -> p o u"))
                nc.vector.quantize_mx(
                    out=w_codes[:, g * CO : (g + 1) * CO].bitcast(FP8X4),
                    scales=w_scales[:, g * CO : (g + 1) * CO],
                    in_=w_bf[:].rearrange("p o u -> p (o u)"),
                )

        def bonus_products(t):
            q = work.tile([P, C], F32)
            nc.gpsimd.tensor_tensor(out=q[:], in0=r_of[t][:], in1=k_of[t][:], op=ALU.mult)
            nc.gpsimd.tensor_tensor(out=q[:], in0=q[:], in1=rk_b[:], op=ALU.mult)
            q_of[t] = q

        def bonus_dot(t):
            dot = stats.tile([P, H], F32)
            nc.vector.tensor_reduce(
                out=dot[:], in_=q_of[t][:].rearrange("p (h c) -> p h c", c=HS), axis=AX.X, op=ALU.add
            )
            dot_of[t] = dot

        def norm_stats(t):
            b, j = norm_where[t]
            if j == 0:
                st = stats.tile([P, GROUP * H * 3], F32)
                st_of[b] = st
            st = st_of[b]
            for a in range(H // 2):
                i0 = (j * (H // 2) + a) * 6
                nc.vector.bn_stats(
                    out=st[:, i0 : i0 + 6],
                    in_=y_of[t][:, a * 2 * HS : (a + 1) * 2 * HS].rearrange("p (h c) -> p c h", h=2),
                )
            if j == NORM_BATCHES[b] - 1:
                nh = NORM_BATCHES[b] * H
                st_v = st[:].rearrange("p (n s) -> p n s", s=3)
                std = stats.tile([P, GROUP * H], F32)
                nc.scalar.activation(
                    out=std[:, :nh], in_=st_v[:, :nh, 2], func=ACTF.Sqrt, bias=eps_t[:, 0:1], scale=1.0 / HS
                )
                negmean = stats.tile([P, GROUP * H], F32)
                nc.scalar.activation(out=negmean[:, :nh], in_=st_v[:, :nh, 1], func=ACTF.Copy, scale=-1.0)
                rstd = stats.tile([P, GROUP * H], F32)
                nc.vector.reciprocal(out=rstd[:, :nh], in_=std[:, :nh])
                shift = stats.tile([P, GROUP * H], F32)
                nc.gpsimd.tensor_tensor(
                    out=shift[:, :nh], in0=negmean[:, :nh], in1=rstd[:, :nh], op=ALU.mult
                )
                rstd_of[b] = rstd
                shift_of[b] = shift

        def transpose_gate_hidden(grp):
            gh_ps = psum.tile([P, GROUP, P], BF16, tag="setup", bufs=1)
            for j in range(GROUP):
                nc.tensor.transpose(gh_ps[:, j, :], gh_of[grp][:, j, :], ident_b[:])
            gh_t = gate.tile([P, GROUP, P], BF16)
            nc.scalar.copy(out=gh_t[:], in_=gh_ps[:])
            ght_of[grp] = gh_t

        def finish_tile(t):
            nb, nj = norm_where[t]
            mb, mj = mx_where[t]
            rstd, shift, dot = rstd_of[nb], shift_of[nb], dot_of[t]
            if mj == 0:
                z_bf = batch.tile([P, GROUP, NPASS, P, PACK], BF16, align_bytes=64)
                z_of[mb] = z_bf
            z_bf = z_of[mb]
            normed = work.tile([P, C], F32)
            bonus = work.tile([P, C], F32)
            for h in range(H):
                col = nj * H + h
                cs = slice(h * HS, (h + 1) * HS)
                nc.scalar.activation(
                    out=normed[:, cs],
                    in_=y_of[t][:, cs],
                    func=ACTF.Identity,
                    bias=shift[:, col : col + 1],
                    scale=rstd[:, col : col + 1],
                )
                nc.scalar.activation(
                    out=bonus[:, cs], in_=v_of[t][:, cs], func=ACTF.Copy, scale=dot[:, h : h + 1]
                )
            for g in range(NPASS):
                normed_ps = psum.tile([P, PACK, P], F32)
                bonus_ps = psum.tile([P, PACK, P], F32)
                g_ps = psum.tile([P, PACK, P], F32)
                for u in range(PACK):
                    blk = g * PACK + u
                    nc.tensor.transpose(normed_ps[:, u, :], normed[:, blk * P : (blk + 1) * P], ident_f[:])
                for u in range(PACK):
                    blk = g * PACK + u
                    nc.tensor.transpose(bonus_ps[:, u, :], bonus[:, blk * P : (blk + 1) * P], ident_f[:])
                for u in range(PACK):
                    blk = g * PACK + u
                    nc.tensor.matmul(
                        g_ps[:, u, :],
                        lhsT=g2_sb[:, blk * P : (blk + 1) * P],
                        rhs=ght_of[t // GROUP][:, t % GROUP, :],
                        start=True,
                        stop=True,
                    )
                affine = work.tile([P, PACK, P], F32)
                for u in range(PACK):
                    blk = g * PACK + u
                    nc.scalar.activation(
                        out=affine[:, u, :],
                        in_=normed_ps[:, u, :],
                        func=ACTF.Identity,
                        bias=ln_cols[:, NBLK + blk : NBLK + blk + 1],
                        scale=ln_cols[:, blk : blk + 1],
                    )
                y2 = work.tile([P, PACK, P], F32)
                nc.vector.tensor_tensor(out=y2[:], in0=affine[:], in1=bonus_ps[:], op=ALU.add)
                nc.vector.tensor_tensor(
                    out=z_bf[:, mj, g],
                    in0=y2[:].rearrange("p u m -> p m u"),
                    in1=g_ps[:].rearrange("p u m -> p m u"),
                    op=ALU.mult,
                )
            if mj == MX_BATCHES[mb] - 1:
                project(mb)

        def project(mb):
            n_tiles = MX_BATCHES[mb]
            words = n_tiles * NPASS * P
            z_codes = batch.tile([P, GROUP * NPASS * P], U32, align_bytes=64)
            z_scales = batch.tile([P, GROUP * NPASS * P], U8, align_bytes=64)
            nc.vector.quantize_mx(
                out=z_codes[:, :words].bitcast(FP8X4),
                scales=z_scales[:, :words],
                in_=z_of[mb][:, :n_tiles].rearrange("p j g m u -> p (j g m u)"),
            )
            o_sb = batch.tile([P, GROUP, CO], F32)
            for j0 in range(0, n_tiles, 2):
                pair = min(2, n_tiles - j0)
                o_ps = psum.tile([P, 2, CO], F32, bufs=1)
                for a in range(pair):
                    for g in range(NPASS):
                        i0 = ((j0 + a) * NPASS + g) * P
                        nc.tensor.matmul_mx(
                            out=o_ps[:, a, :],
                            lhsT=z_codes[:, i0 : i0 + P].bitcast(FP8X4),
                            lhsT_scale=z_scales[:, i0 : i0 + P],
                            rhs=w_codes[:, g * CO : (g + 1) * CO].bitcast(FP8X4),
                            rhs_scale=w_scales[:, g * CO : (g + 1) * CO],
                            start=(g == 0),
                            stop=(g == NPASS - 1),
                        )
                nc.scalar.copy(out=o_sb[:, j0 : j0 + pair, :], in_=o_ps[:, :pair, :])
            t0 = mx_first[mb] * P
            nc.scalar.dma_start(
                out=out_f[t0 : t0 + n_tiles * P, :].rearrange("(j p) o -> p j o", p=P), in_=o_sb[:, :n_tiles, :]
            )

        for slot in range(-STATS_AHEAD, NT):
            if slot >= 0:
                if slot + Y_AHEAD < NT:
                    load_y(slot + Y_AHEAD)
                if slot + RK_AHEAD < NT:
                    load_rk(slot + RK_AHEAD)
                if slot + V_AHEAD < NT:
                    load_v(slot + V_AHEAD)
                if slot % GROUP == 0 and slot + GATE_LOAD_AHEAD < NT:
                    load_gate_hidden((slot + GATE_LOAD_AHEAD) // GROUP)
            if 0 <= slot + PRODUCT_AHEAD < NT:
                bonus_products(slot + PRODUCT_AHEAD)
            if 0 <= slot + STATS_AHEAD < NT:
                norm_stats(slot + STATS_AHEAD)
            if 0 <= slot + DOT_AHEAD < NT:
                bonus_dot(slot + DOT_AHEAD)
            if (slot + GATE_AHEAD) % GROUP == 0 and 0 <= slot + GATE_AHEAD < NT:
                transpose_gate_hidden((slot + GATE_AHEAD) // GROUP)
            if slot == -1:
                quantise_weights()
            if slot >= 0:
                finish_tile(slot)
